import numpy as np
import ml_dtypes


def mxq(x, axis, fmt="e4m3"):
    dtype, down = {"e4m3": (ml_dtypes.float8_e4m3fn, 7), "e5m2": (ml_dtypes.float8_e5m2, 14)}[fmt]
    v = np.moveaxis(np.asarray(x, np.float32).astype(ml_dtypes.bfloat16).astype(np.float64), axis, -1)
    blocks = v.reshape(v.shape[:-1] + (-1, 32))
    amax = np.abs(blocks).max(-1, keepdims=True)
    byte = np.maximum(np.where(amax > 0, np.frexp(amax)[1] - 1 + 127, 0) - down, 1)
    scale = np.exp2(byte - 127.0)
    codes = (blocks / scale).astype(np.float32).astype(dtype).astype(np.float64)
    return np.moveaxis((codes * scale).reshape(v.shape), -1, axis)


WIDE = False


def mx_kscale(k):
    if not WIDE:
        return np.ones(k)
    levels = np.array([10, -10, 5, -5, 0])
    a = np.random.permutation(np.resize(levels, k // 512 * 4)).reshape(k // 512, 4)
    idx = np.arange(k)
    return np.exp2(a[idx // 512, idx % 128 // 32])


BF16 = ml_dtypes.bfloat16


def bf(x):
    return np.asarray(x, np.float32).astype(BF16)


def f64(x):
    return np.asarray(x).astype(np.float64)


B, T, N, D, H = 2, 2, 512, 512, 4
HD = D // H


def split_heads(x):
    return np.moveaxis(x.reshape(B, T, N, H, HD), 3, 0).reshape(H * B, T, N, HD)


def merge_heads(x):
    return np.moveaxis(x.reshape(H, B, T, N, HD), 0, 3).reshape(B, T, N, D)


def setup_inputs():
    s = mx_kscale(D)
    return {"q_heads": bf(np.random.standard_normal((H * B, T, N, HD)) * 1.5),
            "k_heads": bf(np.random.standard_normal((H * B, T, N, HD)) * 1.6),
            "value": bf(np.random.standard_normal((B, T, N, D)) * s),
            "Wv": bf(np.random.standard_normal((D, D)) * 1.5 / np.sqrt(D) / s),
            "bv": bf(np.random.standard_normal(D) * 0.2),
            "dyn": bf(np.random.standard_normal((H * B, T, N, N)) * 0.6),
            "h_gcn": bf(np.maximum(np.random.standard_normal((B, T, N, D)), 0.0))}


def reference(q_heads, k_heads, value, Wv, bv, dyn, h_gcn):
    v2 = split_heads((mxq(f64(value), 3, "e4m3") @ mxq(f64(Wv), 1, "e4m3").T) + f64(bv))
    score = f64(q_heads) @ f64(k_heads).transpose(0, 1, 3, 2) / np.sqrt(HD)
    g = score * f64(dyn)
    e = np.exp(g - g.max(-1, keepdims=True))
    o = (mxq(e, 3, "e4m3") @ mxq(v2, 2, "e4m3")) / e.sum(-1, keepdims=True)
    return 0.5 * f64(h_gcn) + 0.5 * merge_heads(np.tanh(o))

@@ -1,0 +1,277 @@
+import math
+from contextlib import ExitStack
+
+import concourse.mybir as mybir
+from concourse.masks import make_identity
+
+BF16 = mybir.dt.bfloat16
+F32 = mybir.dt.float32
+U32 = mybir.dt.uint32
+U8 = mybir.dt.uint8
+FP8X4 = mybir.dt.float8_e4m3fn_x4
+ALU = mybir.AluOpType
+ACT = mybir.ActivationFunctionType
+AXIS = mybir.AxisListType
+
+P = 128
+B, T, N, D, H = 2, 2, 512, 512, 4
+HD = D // H
+ROW_TILES = N // P
+PACK = 4
+K = 512
+WORDS = K // 2
+BANK = 512
+
+FLOPS = 2 * B * T * N * D * D + 2 * (2 * H * B * T * N * N * HD)
+
+
+def tile_gatedspatialattentionlayer_pb_kernel(
+    tc, q_heads, k_heads, value, Wv, bv, dyn, h_gcn, out
+):
+    nc = tc.nc
+    slices = [(b, t, h) for b in range(B) for t in range(T) for h in range(H)]
+    live = {}
+
+    with ExitStack() as stack:
+        const = stack.enter_context(tc.tile_pool(name="const", bufs=1))
+        loads = stack.enter_context(tc.tile_pool(name="loads", bufs=4))
+        pairs = stack.enter_context(tc.tile_pool(name="pairs", bufs=2))
+        work = stack.enter_context(tc.tile_pool(name="work", bufs=3))
+        logits = stack.enter_context(tc.tile_pool(name="logits", bufs=6))
+        ps_score = stack.enter_context(tc.psum_pool(name="ps_score", bufs=3))
+        ps_words = stack.enter_context(tc.psum_pool(name="ps_words", bufs=2))
+        ps_single = stack.enter_context(tc.psum_pool(name="ps_single", bufs=1))
+
+        ident_bf16 = const.tile([P, P], BF16, name="ident_bf16")
+        make_identity(nc, ident_bf16[:])
+        ident_f32 = const.tile([P, P], F32, name="ident_f32")
+        make_identity(nc, ident_f32[:])
+
+        zero = const.tile([P, 1], F32, name="zero")
+        nc.vector.memset(zero[:], 0.0)
+        one = const.tile([P, 1], F32, name="one")
+        nc.scalar.activation(out=one[:], in_=zero[:], func=ACT.Exp)
+
+        def rows_to_codes(rows, codes, scales):
+            words = rows.bitcast(F32)
+            grouped = work.tile([P, ROW_TILES * P * PACK], BF16, name="grouped", align_bytes=64)
+            for half in range(2):
+                bank = ps_words.tile([P, BANK], F32, name="wordsT")
+                spots = bank[:].rearrange("p (i r u) -> p i r u", i=2, u=2)
+                for i in range(2):
+                    for u in range(2):
+                        first = (2 * half + i) * WORDS + u * P
+                        nc.tensor.transpose(
+                            out=spots[:, i, :, u],
+                            in_=words[:, first : first + P],
+                            identity=ident_f32[:],
+                        )
+                nc.scalar.copy(
+                    out=grouped[:, half * 2 * BANK : (half + 1) * 2 * BANK],
+                    in_=bank[:].bitcast(BF16),
+                )
+            nc.vector.quantize_mx(out=codes.bitcast(FP8X4), scales=scales, in_=grouped[:])
+
+        def load_slice(s):
+            b, t, h = slices[s]
+            hb = h * B + b
+            q_rows = loads.tile([P, ROW_TILES * HD], BF16, name="q_rows")
+            nc.sync.dma_start(
+                out=q_rows[:], in_=q_heads[hb, t].rearrange("(p j) d -> p (j d)", j=ROW_TILES)
+            )
+            k_rows = loads.tile([P, ROW_TILES * HD], BF16, name="k_rows")
+            nc.sync.dma_start(
+                out=k_rows[:].rearrange("p (j d) -> p j d", j=ROW_TILES),
+                in_=k_heads[hb, t].rearrange("(j p) d -> p j d", p=P),
+            )
+            gate = loads.tile([P, ROW_TILES * N], BF16, name="gate")
+            nc.sync.dma_start(
+                out=gate[:], in_=dyn[hb, t].rearrange("(p j) k -> p (j k)", j=ROW_TILES)
+            )
+            live["q_rows", s], live["k_rows", s], live["gate", s] = q_rows, k_rows, gate
+
+        def load_weights():
+            w_rows = pairs.tile([P, ROW_TILES * K], BF16, name="rows")
+            nc.sync.dma_start(
+                out=w_rows[:].rearrange("p (i k) -> p i k", i=ROW_TILES),
+                in_=Wv.rearrange("(i p) k -> p i k", p=P),
+            )
+            live["w_rows"] = w_rows
+
+        def load_bias():
+            bias = const.tile([P, D], BF16, name="bias")
+            nc.sync.dma_start(out=bias[:], in_=bv.partition_broadcast(P))
+            live["bias"] = bias
+
+        def load_pair(b, t):
+            v_rows = pairs.tile([P, ROW_TILES * K], BF16, name="rows")
+            nc.sync.dma_start(
+                out=v_rows[:].rearrange("p (u x) -> p u x", u=2),
+                in_=value[b, t].rearrange("(u p e) d -> p u (e d)", u=2, e=2),
+            )
+            h_rows = pairs.tile([P, ROW_TILES * D], BF16, name="h_rows")
+            nc.sync.dma_start(
+                out=h_rows[:], in_=h_gcn[b, t].rearrange("(p j) d -> p (j d)", j=ROW_TILES)
+            )
+            live["v_rows", b, t], live["h_rows", b, t] = v_rows, h_rows
+
+        def quantise_weights():
+            w_codes = const.tile([P, D], U32, name="w_codes", align_bytes=64)
+            w_scales = const.tile([P, D], U8, name="w_scales", align_bytes=64)
+            rows_to_codes(live["w_rows"][:], w_codes[:], w_scales[:])
+            live["w_codes"], live["w_scales"] = w_codes, w_scales
+
+        def quantise_value(b, t):
+            x_codes = pairs.tile([P, N], U32, name="x_codes", align_bytes=64)
+            x_scales = pairs.tile([P, N], U8, name="x_scales", align_bytes=64)
+            rows_to_codes(live["v_rows", b, t][:], x_codes[:], x_scales[:])
+            live["x_codes", b, t], live["x_scales", b, t] = x_codes, x_scales
+
+        def project_value(s):
+            b, t, h = slices[s]
+            head = slice(h * HD, (h + 1) * HD)
+            v_bank = ps_single.tile([P, PACK * HD], F32, name="v_bank")
+            for i in range(PACK):
+                nodes = slice(i * P, (i + 1) * P)
+                nc.tensor.matmul_mx(
+                    out=v_bank[:, i * HD : (i + 1) * HD],
+                    lhsT=live["x_codes", b, t][:, nodes].bitcast(FP8X4),
+                    lhsT_scale=live["x_scales", b, t][:, nodes],
+                    rhs=live["w_codes"][:, head].bitcast(FP8X4),
+                    rhs_scale=live["w_scales"][:, head],
+                    start=True,
+                    stop=True,
+                )
+            v_grouped = work.tile([P, HD * PACK], BF16, name="v_grouped", align_bytes=64)
+            nc.vector.tensor_tensor(
+                out=v_grouped[:].rearrange("p (c i) -> p c i", i=PACK),
+                in0=v_bank[:].rearrange("p (i c) -> p c i", i=PACK),
+                in1=live["bias"][:, head].unsqueeze(2).to_broadcast([P, HD, PACK]),
+                op=ALU.add,
+            )
+            v_codes = work.tile([P, HD], U32, name="v_codes", bufs=4, align_bytes=64)
+            v_scales = work.tile([P, HD], U8, name="v_scales", bufs=4, align_bytes=64)
+            nc.vector.quantize_mx(
+                out=v_codes[:].bitcast(FP8X4), scales=v_scales[:], in_=v_grouped[:]
+            )
+            live["v_codes", s], live["v_scales", s] = v_codes, v_scales
+
+        def transpose_q_and_k(s):
+            qkT_bank = ps_single.tile([P, 2 * N], BF16, name="qkT_bank")
+            for j in range(ROW_TILES):
+                nc.tensor.transpose(
+                    out=qkT_bank[:, j * P : (j + 1) * P],
+                    in_=live["q_rows", s][:, j * HD : (j + 1) * HD],
+                    identity=ident_bf16[:],
+                )
+            for j in range(ROW_TILES):
+                nc.tensor.transpose(
+                    out=qkT_bank[:, N + j * P : N + (j + 1) * P],
+                    in_=live["k_rows", s][:, j * HD : (j + 1) * HD],
+                    identity=ident_bf16[:],
+                )
+            qkT = work.tile([P, 2 * N], BF16, name="qkT")
+            nc.scalar.copy(out=qkT[:], in_=qkT_bank[:])
+            live["qkT", s] = qkT
+
+        def gated_softmax(s):
+            qkT, gate = live["qkT", s], live["gate", s]
+            e_rows = work.tile([P, ROW_TILES * N], BF16, name="e_rows")
+            neg_max = work.tile([P, ROW_TILES], F32, name="neg_max")
+            row_sum = work.tile([P, ROW_TILES], F32, name="row_sum")
+            for j in range(ROW_TILES):
+                keys = slice(j * N, (j + 1) * N)
+                score = ps_score.tile([P, N], F32, name="score")
+                nc.tensor.matmul(
+                    out=score[:],
+                    lhsT=qkT[:, j * P : (j + 1) * P],
+                    rhs=qkT[:, N : 2 * N],
+                    start=True,
+                    stop=True,
+                )
+                g = logits.tile([P, N], F32, name="g")
+                nc.vector.scalar_tensor_tensor(
+                    out=g[:],
+                    in0=score[:],
+                    scalar=1.0 / math.sqrt(HD),
+                    in1=gate[:, keys],
+                    op0=ALU.mult,
+                    op1=ALU.mult,
+                )
+                nc.vector.tensor_reduce(
+                    out=neg_max[:, j : j + 1], in_=g[:], axis=AXIS.X, op=ALU.max, negate=True
+                )
+                nc.scalar.activation(
+                    out=e_rows[:, keys],
+                    in_=g[:],
+                    func=ACT.Exp,
+                    bias=neg_max[:, j : j + 1],
+                    scale=1.0,
+                    accum_out=row_sum[:, j : j + 1],
+                )
+            live["e_rows", s], live["row_sum", s] = e_rows, row_sum
+
+        def attend(s):
+            b, t, h = slices[s]
+            e_codes = work.tile([P, N], U32, name="e_codes", align_bytes=64)
+            e_scales = work.tile([P, N], U8, name="e_scales", align_bytes=64)
+            rows_to_codes(live["e_rows", s][:], e_codes[:], e_scales[:])
+            o_bank = ps_single.tile([P, ROW_TILES * HD], F32, name="o_bank")
+            for j in range(ROW_TILES):
+                queries = slice(j * P, (j + 1) * P)
+                nc.tensor.matmul_mx(
+                    out=o_bank[:, j * HD : (j + 1) * HD],
+                    lhsT=e_codes[:, queries].bitcast(FP8X4),
+                    lhsT_scale=e_scales[:, queries],
+                    rhs=live["v_codes", s][:].bitcast(FP8X4),
+                    rhs_scale=live["v_scales", s][:],
+                    start=True,
+                    stop=True,
+                )
+            inv_sum = work.tile([P, ROW_TILES], F32, name="inv_sum")
+            nc.vector.reciprocal(out=inv_sum[:], in_=live["row_sum", s][:])
+            if h == 0:
+                live["result", b, t] = pairs.tile([P, ROW_TILES * D], F32, name="result")
+            result = live["result", b, t]
+            for j in range(ROW_TILES):
+                nc.scalar.activation(
+                    out=result[:, j * D + h * HD : j * D + (h + 1) * HD],
+                    in_=o_bank[:, j * HD : (j + 1) * HD],
+                    func=ACT.Tanh,
+                    scale=inv_sum[:, j : j + 1],
+                )
+            head = slice(h * HD, (h + 1) * HD)
+            mine = result[:].rearrange("p (j d) -> p j d", j=ROW_TILES)[:, :, head]
+            other = live["h_rows", b, t][:].rearrange("p (j d) -> p j d", j=ROW_TILES)[:, :, head]
+            nc.gpsimd.tensor_tensor(out=mine, in0=mine, in1=other, op=ALU.add)
+            nc.gpsimd.tensor_scalar(
+                out=mine, in0=mine, scalar1=0.5, scalar2=0.0, op0=ALU.mult, op1=ALU.add
+            )
+            if h == H - 1:
+                nc.sync.dma_start(
+                    out=out[b, t].rearrange("(p j) d -> p (j d)", j=ROW_TILES), in_=result[:]
+                )
+
+        def prepare(s):
+            b, t, h = slices[s]
+            load_slice(s)
+            if s == 0:
+                load_weights()
+            if h == 0:
+                load_pair(b, t)
+            if s == 0:
+                load_bias()
+            transpose_q_and_k(s)
+            if s == 0:
+                quantise_weights()
+            if h == 0:
+                quantise_value(b, t)
+            project_value(s)
+
+        for step in range(len(slices) + 2):
+            if step >= 2:
+                attend(step - 2)
+            if 1 <= step <= len(slices):
+                gated_softmax(step - 1)
+            if step < len(slices):
+                prepare(step)

@@ -30,7 +30,15 @@ def tile_gatedspatialattentionlayer_pb_kernel(
 ):
     nc = tc.nc
     slices = [(b, t, h) for b in range(B) for t in range(T) for h in range(H)]
+    n_slices = len(slices)
+    n_tiles = n_slices * ROW_TILES
     live = {}
+
+    def is_slice(s):
+        return 0 <= s < n_slices
+
+    def starts_pair(s):
+        return is_slice(s) and s % H == 0
 
     with ExitStack() as stack:
         const = stack.enter_context(tc.tile_pool(name="const", bufs=1))
@@ -41,6 +49,7 @@ def tile_gatedspatialattentionlayer_pb_kernel(
         ps_score = stack.enter_context(tc.psum_pool(name="ps_score", bufs=3))
         ps_words = stack.enter_context(tc.psum_pool(name="ps_words", bufs=2))
         ps_single = stack.enter_context(tc.psum_pool(name="ps_single", bufs=1))
+        stack.enter_context(tc.manual_schedule())
 
         ident_bf16 = const.tile([P, P], BF16, name="ident_bf16")
         make_identity(nc, ident_bf16[:])
@@ -52,43 +61,27 @@ def tile_gatedspatialattentionlayer_pb_kernel(
         one = const.tile([P, 1], F32, name="one")
         nc.scalar.activation(out=one[:], in_=zero[:], func=ACT.Exp)
 
-        def rows_to_codes(rows, codes, scales):
-            words = rows.bitcast(F32)
-            grouped = work.tile([P, ROW_TILES * P * PACK], BF16, name="grouped", align_bytes=64)
-            for half in range(2):
-                bank = ps_words.tile([P, BANK], F32, name="wordsT")
-                spots = bank[:].rearrange("p (i r u) -> p i r u", i=2, u=2)
-                for i in range(2):
-                    for u in range(2):
-                        first = (2 * half + i) * WORDS + u * P
-                        nc.tensor.transpose(
-                            out=spots[:, i, :, u],
-                            in_=words[:, first : first + P],
-                            identity=ident_f32[:],
-                        )
-                nc.scalar.copy(
-                    out=grouped[:, half * 2 * BANK : (half + 1) * 2 * BANK],
-                    in_=bank[:].bitcast(BF16),
-                )
-            nc.vector.quantize_mx(out=codes.bitcast(FP8X4), scales=scales, in_=grouped[:])
-
-        def load_slice(s):
+        def load_q_and_k(s):
             b, t, h = slices[s]
-            hb = h * B + b
             q_rows = loads.tile([P, ROW_TILES * HD], BF16, name="q_rows")
             nc.sync.dma_start(
-                out=q_rows[:], in_=q_heads[hb, t].rearrange("(p j) d -> p (j d)", j=ROW_TILES)
+                out=q_rows[:],
+                in_=q_heads[h * B + b, t].rearrange("(p j) d -> p (j d)", j=ROW_TILES),
             )
             k_rows = loads.tile([P, ROW_TILES * HD], BF16, name="k_rows")
             nc.sync.dma_start(
                 out=k_rows[:].rearrange("p (j d) -> p j d", j=ROW_TILES),
-                in_=k_heads[hb, t].rearrange("(j p) d -> p j d", p=P),
+                in_=k_heads[h * B + b, t].rearrange("(j p) d -> p j d", p=P),
             )
+            live["q_rows", s], live["k_rows", s] = q_rows, k_rows
+
+        def load_gate(s):
+            b, t, h = slices[s]
             gate = loads.tile([P, ROW_TILES * N], BF16, name="gate")
             nc.sync.dma_start(
-                out=gate[:], in_=dyn[hb, t].rearrange("(p j) k -> p (j k)", j=ROW_TILES)
+                out=gate[:], in_=dyn[h * B + b, t].rearrange("(p j) k -> p (j k)", j=ROW_TILES)
             )
-            live["q_rows", s], live["k_rows", s], live["gate", s] = q_rows, k_rows, gate
+            live["gate", s] = gate
 
         def load_weights():
             w_rows = pairs.tile([P, ROW_TILES * K], BF16, name="rows")
@@ -96,67 +89,128 @@ def tile_gatedspatialattentionlayer_pb_kernel(
                 out=w_rows[:].rearrange("p (i k) -> p i k", i=ROW_TILES),
                 in_=Wv.rearrange("(i p) k -> p i k", p=P),
             )
-            live["w_rows"] = w_rows
+            live["rows", "w"] = w_rows
 
         def load_bias():
             bias = const.tile([P, D], BF16, name="bias")
             nc.sync.dma_start(out=bias[:], in_=bv.partition_broadcast(P))
             live["bias"] = bias
 
-        def load_pair(b, t):
+        def load_value(s):
+            b, t, h = slices[s]
             v_rows = pairs.tile([P, ROW_TILES * K], BF16, name="rows")
             nc.sync.dma_start(
                 out=v_rows[:].rearrange("p (u x) -> p u x", u=2),
                 in_=value[b, t].rearrange("(u p e) d -> p u (e d)", u=2, e=2),
             )
+            live["rows", "x", s] = v_rows
+
+        def load_h(s):
+            b, t, h = slices[s]
             h_rows = pairs.tile([P, ROW_TILES * D], BF16, name="h_rows")
             nc.sync.dma_start(
                 out=h_rows[:], in_=h_gcn[b, t].rearrange("(p j) d -> p (j d)", j=ROW_TILES)
             )
-            live["v_rows", b, t], live["h_rows", b, t] = v_rows, h_rows
+            live["h_rows", b, t] = h_rows
+
+        def transpose_words(rows, half):
+            words = rows[:].bitcast(F32)
+            bank = ps_words.tile([P, BANK], F32, name="wordsT")
+            spots = bank[:].rearrange("p (i r u) -> p i r u", i=2, u=2)
+            for i in range(2):
+                for u in range(2):
+                    first = (2 * half + i) * WORDS + u * P
+                    nc.tensor.transpose(
+                        out=spots[:, i, :, u],
+                        in_=words[:, first : first + P],
+                        identity=ident_f32[:],
+                    )
+            return bank
+
+        def copy_words(bank, grouped, half):
+            nc.scalar.copy(
+                out=grouped[:, half * 2 * BANK : (half + 1) * 2 * BANK], in_=bank[:].bitcast(BF16)
+            )
+
+        def new_grouped():
+            return work.tile([P, ROW_TILES * P * PACK], BF16, name="grouped", align_bytes=64)
+
+        def quantise(grouped, codes, scales):
+            nc.vector.quantize_mx(out=codes[:].bitcast(FP8X4), scales=scales[:], in_=grouped[:])
+
+        def transpose_weights(half):
+            live["bank", "w", half] = transpose_words(live["rows", "w"], half)
+
+        def copy_weights(half):
+            if half == 0:
+                live["grouped", "w"] = new_grouped()
+            copy_words(live["bank", "w", half], live["grouped", "w"], half)
 
         def quantise_weights():
             w_codes = const.tile([P, D], U32, name="w_codes", align_bytes=64)
             w_scales = const.tile([P, D], U8, name="w_scales", align_bytes=64)
-            rows_to_codes(live["w_rows"][:], w_codes[:], w_scales[:])
+            quantise(live["grouped", "w"], w_codes, w_scales)
             live["w_codes"], live["w_scales"] = w_codes, w_scales
 
-        def quantise_value(b, t):
-            x_codes = pairs.tile([P, N], U32, name="x_codes", align_bytes=64)
-            x_scales = pairs.tile([P, N], U8, name="x_scales", align_bytes=64)
-            rows_to_codes(live["v_rows", b, t][:], x_codes[:], x_scales[:])
-            live["x_codes", b, t], live["x_scales", b, t] = x_codes, x_scales
+        def transpose_value(s, half):
+            if starts_pair(s):
+                live["bank", "x", half] = transpose_words(live["rows", "x", s], half)
+
+        def copy_value(s, half):
+            if starts_pair(s):
+                if half == 0:
+                    live["grouped", "x"] = new_grouped()
+                copy_words(live["bank", "x", half], live["grouped", "x"], half)
+
+        def quantise_value(s):
+            if starts_pair(s):
+                x_codes = pairs.tile([P, N], U32, name="x_codes", align_bytes=64)
+                x_scales = pairs.tile([P, N], U8, name="x_scales", align_bytes=64)
+                quantise(live["grouped", "x"], x_codes, x_scales)
+                live["x_codes", s // H], live["x_scales", s // H] = x_codes, x_scales
 
         def project_value(s):
-            b, t, h = slices[s]
-            head = slice(h * HD, (h + 1) * HD)
+            if not is_slice(s):
+                return
+            head = slice((s % H) * HD, (s % H + 1) * HD)
             v_bank = ps_single.tile([P, PACK * HD], F32, name="v_bank")
             for i in range(PACK):
                 nodes = slice(i * P, (i + 1) * P)
                 nc.tensor.matmul_mx(
                     out=v_bank[:, i * HD : (i + 1) * HD],
-                    lhsT=live["x_codes", b, t][:, nodes].bitcast(FP8X4),
-                    lhsT_scale=live["x_scales", b, t][:, nodes],
+                    lhsT=live["x_codes", s // H][:, nodes].bitcast(FP8X4),
+                    lhsT_scale=live["x_scales", s // H][:, nodes],
                     rhs=live["w_codes"][:, head].bitcast(FP8X4),
                     rhs_scale=live["w_scales"][:, head],
                     start=True,
                     stop=True,
                 )
+            live["v_bank", s] = v_bank
+
+        def add_bias(s):
+            if not is_slice(s):
+                return
+            head = slice((s % H) * HD, (s % H + 1) * HD)
             v_grouped = work.tile([P, HD * PACK], BF16, name="v_grouped", align_bytes=64)
             nc.vector.tensor_tensor(
                 out=v_grouped[:].rearrange("p (c i) -> p c i", i=PACK),
-                in0=v_bank[:].rearrange("p (i c) -> p c i", i=PACK),
+                in0=live["v_bank", s][:].rearrange("p (i c) -> p c i", i=PACK),
                 in1=live["bias"][:, head].unsqueeze(2).to_broadcast([P, HD, PACK]),
                 op=ALU.add,
             )
-            v_codes = work.tile([P, HD], U32, name="v_codes", bufs=4, align_bytes=64)
-            v_scales = work.tile([P, HD], U8, name="v_scales", bufs=4, align_bytes=64)
-            nc.vector.quantize_mx(
-                out=v_codes[:].bitcast(FP8X4), scales=v_scales[:], in_=v_grouped[:]
-            )
+            live["v_grouped", s] = v_grouped
+
+        def quantise_v(s):
+            if not is_slice(s):
+                return
+            v_codes = work.tile([P, HD], U32, name="v_codes", align_bytes=64)
+            v_scales = work.tile([P, HD], U8, name="v_scales", align_bytes=64)
+            quantise(live["v_grouped", s], v_codes, v_scales)
             live["v_codes", s], live["v_scales", s] = v_codes, v_scales
 
         def transpose_q_and_k(s):
+            if not is_slice(s):
+                return
             qkT_bank = ps_single.tile([P, 2 * N], BF16, name="qkT_bank")
             for j in range(ROW_TILES):
                 nc.tensor.transpose(
@@ -170,108 +224,205 @@ def tile_gatedspatialattentionlayer_pb_kernel(
                     in_=live["k_rows", s][:, j * HD : (j + 1) * HD],
                     identity=ident_bf16[:],
                 )
+            live["qkT_bank", s] = qkT_bank
+
+        def copy_q_and_k(s):
+            if not is_slice(s):
+                return
             qkT = work.tile([P, 2 * N], BF16, name="qkT")
-            nc.scalar.copy(out=qkT[:], in_=qkT_bank[:])
+            nc.scalar.copy(out=qkT[:], in_=live["qkT_bank", s][:])
             live["qkT", s] = qkT
 
-        def gated_softmax(s):
-            qkT, gate = live["qkT", s], live["gate", s]
-            e_rows = work.tile([P, ROW_TILES * N], BF16, name="e_rows")
-            neg_max = work.tile([P, ROW_TILES], F32, name="neg_max")
-            row_sum = work.tile([P, ROW_TILES], F32, name="row_sum")
-            for j in range(ROW_TILES):
-                keys = slice(j * N, (j + 1) * N)
-                score = ps_score.tile([P, N], F32, name="score")
-                nc.tensor.matmul(
-                    out=score[:],
-                    lhsT=qkT[:, j * P : (j + 1) * P],
-                    rhs=qkT[:, N : 2 * N],
-                    start=True,
-                    stop=True,
-                )
-                g = logits.tile([P, N], F32, name="g")
-                nc.vector.scalar_tensor_tensor(
-                    out=g[:],
-                    in0=score[:],
-                    scalar=1.0 / math.sqrt(HD),
-                    in1=gate[:, keys],
-                    op0=ALU.mult,
-                    op1=ALU.mult,
-                )
-                nc.vector.tensor_reduce(
-                    out=neg_max[:, j : j + 1], in_=g[:], axis=AXIS.X, op=ALU.max, negate=True
-                )
-                nc.scalar.activation(
-                    out=e_rows[:, keys],
-                    in_=g[:],
-                    func=ACT.Exp,
-                    bias=neg_max[:, j : j + 1],
-                    scale=1.0,
-                    accum_out=row_sum[:, j : j + 1],
-                )
-            live["e_rows", s], live["row_sum", s] = e_rows, row_sum
+        def score(tile):
+            if not 0 <= tile < n_tiles:
+                return
+            s, j = divmod(tile, ROW_TILES)
+            bank = ps_score.tile([P, N], F32, name="score")
+            nc.tensor.matmul(
+                out=bank[:],
+                lhsT=live["qkT", s][:, j * P : (j + 1) * P],
+                rhs=live["qkT", s][:, N : 2 * N],
+                start=True,
+                stop=True,
+            )
+            live["score", tile] = bank
+
+        def gate_scores(tile):
+            if not 0 <= tile < n_tiles:
+                return
+            s, j = divmod(tile, ROW_TILES)
+            g = logits.tile([P, N], F32, name="g")
+            nc.vector.scalar_tensor_tensor(
+                out=g[:],
+                in0=live["score", tile][:],
+                scalar=1.0 / math.sqrt(HD),
+                in1=live["gate", s][:, j * N : (j + 1) * N],
+                op0=ALU.mult,
+                op1=ALU.mult,
+            )
+            live["g", tile] = g
+
+        def row_max(tile):
+            if not 0 <= tile < n_tiles:
+                return
+            s, j = divmod(tile, ROW_TILES)
+            if j == 0:
+                live["neg_max", s] = work.tile([P, ROW_TILES], F32, name="neg_max")
+            nc.vector.tensor_reduce(
+                out=live["neg_max", s][:, j : j + 1],
+                in_=live["g", tile][:],
+                axis=AXIS.X,
+                op=ALU.max,
+                negate=True,
+            )
+
+        def exponentials(tile):
+            if not 0 <= tile < n_tiles:
+                return
+            s, j = divmod(tile, ROW_TILES)
+            if j == 0:
+                live["rows", "e", s] = work.tile([P, ROW_TILES * N], BF16, name="e_rows")
+                live["row_sum", s] = work.tile([P, ROW_TILES], F32, name="row_sum")
+            nc.scalar.activation(
+                out=live["rows", "e", s][:, j * N : (j + 1) * N],
+                in_=live["g", tile][:],
+                func=ACT.Exp,
+                bias=live["neg_max", s][:, j : j + 1],
+                scale=1.0,
+                accum_out=live["row_sum", s][:, j : j + 1],
+            )
+
+        def transpose_e(s, half):
+            if is_slice(s):
+                live["bank", "e", s, half] = transpose_words(live["rows", "e", s], half)
+
+        def copy_e(s, half):
+            if is_slice(s):
+                if half == 0:
+                    live["grouped", "e", s] = new_grouped()
+                copy_words(live["bank", "e", s, half], live["grouped", "e", s], half)
+
+        def quantise_e(s):
+            if is_slice(s):
+                e_codes = work.tile([P, N], U32, name="e_codes", align_bytes=64)
+                e_scales = work.tile([P, N], U8, name="e_scales", align_bytes=64)
+                quantise(live["grouped", "e", s], e_codes, e_scales)
+                live["e_codes", s], live["e_scales", s] = e_codes, e_scales
 
         def attend(s):
-            b, t, h = slices[s]
-            e_codes = work.tile([P, N], U32, name="e_codes", align_bytes=64)
-            e_scales = work.tile([P, N], U8, name="e_scales", align_bytes=64)
-            rows_to_codes(live["e_rows", s][:], e_codes[:], e_scales[:])
+            if not is_slice(s):
+                return
             o_bank = ps_single.tile([P, ROW_TILES * HD], F32, name="o_bank")
             for j in range(ROW_TILES):
                 queries = slice(j * P, (j + 1) * P)
                 nc.tensor.matmul_mx(
                     out=o_bank[:, j * HD : (j + 1) * HD],
-                    lhsT=e_codes[:, queries].bitcast(FP8X4),
-                    lhsT_scale=e_scales[:, queries],
+                    lhsT=live["e_codes", s][:, queries].bitcast(FP8X4),
+                    lhsT_scale=live["e_scales", s][:, queries],
                     rhs=live["v_codes", s][:].bitcast(FP8X4),
                     rhs_scale=live["v_scales", s][:],
                     start=True,
                     stop=True,
                 )
+            live["o_bank", s] = o_bank
+
+        def invert_sums(s):
+            if not is_slice(s):
+                return
             inv_sum = work.tile([P, ROW_TILES], F32, name="inv_sum")
             nc.vector.reciprocal(out=inv_sum[:], in_=live["row_sum", s][:])
-            if h == 0:
-                live["result", b, t] = pairs.tile([P, ROW_TILES * D], F32, name="result")
-            result = live["result", b, t]
+            live["inv_sum", s] = inv_sum
+
+        def finish(s):
+            if not is_slice(s):
+                return
+            b, t, h = slices[s]
+            head = slice(h * HD, (h + 1) * HD)
+            result = work.tile([P, ROW_TILES * HD], F32, name="result")
             for j in range(ROW_TILES):
                 nc.scalar.activation(
-                    out=result[:, j * D + h * HD : j * D + (h + 1) * HD],
-                    in_=o_bank[:, j * HD : (j + 1) * HD],
+                    out=result[:, j * HD : (j + 1) * HD],
+                    in_=live["o_bank", s][:, j * HD : (j + 1) * HD],
                     func=ACT.Tanh,
-                    scale=inv_sum[:, j : j + 1],
+                    scale=live["inv_sum", s][:, j : j + 1],
                 )
-            head = slice(h * HD, (h + 1) * HD)
-            mine = result[:].rearrange("p (j d) -> p j d", j=ROW_TILES)[:, :, head]
+            by_tile = result[:].rearrange("p (j c) -> p j c", j=ROW_TILES)
             other = live["h_rows", b, t][:].rearrange("p (j d) -> p j d", j=ROW_TILES)[:, :, head]
-            nc.gpsimd.tensor_tensor(out=mine, in0=mine, in1=other, op=ALU.add)
+            nc.gpsimd.tensor_tensor(out=by_tile, in0=by_tile, in1=other, op=ALU.add)
             nc.gpsimd.tensor_scalar(
-                out=mine, in0=mine, scalar1=0.5, scalar2=0.0, op0=ALU.mult, op1=ALU.add
+                out=result[:], in0=result[:], scalar1=0.5, scalar2=0.0, op0=ALU.mult, op1=ALU.add
             )
-            if h == H - 1:
-                nc.sync.dma_start(
-                    out=out[b, t].rearrange("(p j) d -> p (j d)", j=ROW_TILES), in_=result[:]
-                )
+            nc.sync.dma_start(
+                out=out[b, t].rearrange("(p j) d -> p j d", j=ROW_TILES)[:, :, head], in_=by_tile
+            )
 
-        def prepare(s):
-            b, t, h = slices[s]
-            load_slice(s)
-            if s == 0:
-                load_weights()
-            if h == 0:
-                load_pair(b, t)
-            if s == 0:
-                load_bias()
-            transpose_q_and_k(s)
-            if s == 0:
+        load_q_and_k(0)
+        load_gate(0)
+        load_q_and_k(1)
+        load_weights()
+        load_value(0)
+        load_bias()
+        load_gate(1)
+        load_q_and_k(2)
+        load_gate(2)
+        load_h(0)
+
+        first_step = -ROW_TILES - 2
+        last_step = n_tiles + ROW_TILES + 2
+        for step in range(first_step, last_step + 1):
+            cur, j = divmod(step, ROW_TILES)
+
+            if j == 0 and cur >= 0 and is_slice(cur + 3):
+                load_q_and_k(cur + 3)
+                load_gate(cur + 3)
+            if j == 0 and starts_pair(cur + 2) and cur >= 0:
+                load_value(cur + 2)
+                load_h(cur + 2)
+
+            if j == 0:
+                score(step + 2)
+                attend(cur - 2)
+                score(step + 3)
+                transpose_e(cur - 1, 1)
+                transpose_value(cur, 0)
+            if j == 2:
+                score(step + 2)
+                project_value(cur - 1)
+                score(step + 3)
+                transpose_e(cur, 0)
+                transpose_q_and_k(cur + 2)
+                transpose_value(cur, 1)
+            if step == -2:
+                transpose_weights(0)
+            if step == 0:
+                transpose_weights(1)
+
+            if j == 0:
+                copy_q_and_k(cur + 1)
+            if j == 1:
+                copy_e(cur - 1, 1)
+                copy_value(cur, 0)
+            if j == 2:
+                finish(cur - 2)
+            if j == 3:
+                copy_e(cur, 0)
+                copy_value(cur, 1)
+            if step == -1:
+                copy_weights(0)
+            if step == 1:
+                copy_weights(1)
+
+            gate_scores(step + 1)
+            row_max(step)
+            if j == 0:
+                quantise_value(cur - 1)
+            if j == 2:
+                quantise_e(cur - 1)
+                add_bias(cur - 1)
+            if j == 3:
+                quantise_v(cur - 1)
+                invert_sums(cur - 1)
+            if step == 3:
                 quantise_weights()
-            if h == 0:
-                quantise_value(b, t)
-            project_value(s)
 
-        for step in range(len(slices) + 2):
-            if step >= 2:
-                attend(step - 2)
-            if 1 <= step <= len(slices):
-                gated_softmax(step - 1)
-            if step < len(slices):
-                prepare(step)
+            exponentials(step)

@@ -116,21 +116,24 @@ def tile_gatedspatialattentionlayer_pb_kernel(
         def transpose_words(rows, half):
             words = rows[:].bitcast(F32)
             bank = ps_words.tile([P, BANK], F32, name="wordsT")
-            spots = bank[:].rearrange("p (i r u) -> p i r u", i=2, u=2)
-            for i in range(2):
-                for u in range(2):
-                    first = (2 * half + i) * WORDS + u * P
-                    nc.tensor.transpose(
-                        out=spots[:, i, :, u],
-                        in_=words[:, first : first + P],
-                        identity=ident_f32[:],
-                    )
+            for part in range(2 * 2):
+                first = 2 * half * WORDS + part * P
+                nc.tensor.transpose(
+                    out=bank[:, part * P : (part + 1) * P],
+                    in_=words[:, first : first + P],
+                    identity=ident_f32[:],
+                )
             return bank
 
         def copy_words(bank, grouped, half):
-            nc.scalar.copy(
-                out=grouped[:, half * 2 * BANK : (half + 1) * 2 * BANK], in_=bank[:].bitcast(BF16)
-            )
+            for i in range(2):
+                tile_columns = slice((2 * half + i) * P * PACK, (2 * half + i + 1) * P * PACK)
+                nc.scalar.copy(
+                    out=grouped[:, tile_columns].rearrange("p (r u e) -> p r u e", u=2, e=2),
+                    in_=bank[:]
+                    .bitcast(BF16)[:, i * P * PACK : (i + 1) * P * PACK]
+                    .rearrange("p (u r e) -> p r u e", u=2, e=2),
+                )
 
         def new_grouped():
             return work.tile([P, ROW_TILES * P * PACK], BF16, name="grouped", align_bytes=64)

@@ -126,14 +126,11 @@ def tile_gatedspatialattentionlayer_pb_kernel(
             return bank
 
         def copy_words(bank, grouped, half):
-            for i in range(2):
-                tile_columns = slice((2 * half + i) * P * PACK, (2 * half + i + 1) * P * PACK)
-                nc.scalar.copy(
-                    out=grouped[:, tile_columns].rearrange("p (r u e) -> p r u e", u=2, e=2),
-                    in_=bank[:]
-                    .bitcast(BF16)[:, i * P * PACK : (i + 1) * P * PACK]
-                    .rearrange("p (u r e) -> p r u e", u=2, e=2),
-                )
+            columns = slice(2 * half * P * PACK, 2 * (half + 1) * P * PACK)
+            nc.scalar.copy(
+                out=grouped[:, columns].bitcast(F32).rearrange("p (i r u) -> p i r u", i=2, u=2),
+                in_=bank[:].rearrange("p (i u r) -> p i r u", i=2, u=2),
+            )
 
         def new_grouped():
             return work.tile([P, ROW_TILES * P * PACK], BF16, name="grouped", align_bytes=64)

@@ -153,21 +153,18 @@ def tile_gatedspatialattentionlayer_pb_kernel(
             live["w_codes"], live["w_scales"] = w_codes, w_scales
 
         def transpose_value(s, half):
-            if starts_pair(s):
-                live["bank", "x", half] = transpose_words(live["rows", "x", s], half)
+            live["bank", "x", half] = transpose_words(live["rows", "x", s], half)
 
-        def copy_value(s, half):
-            if starts_pair(s):
-                if half == 0:
-                    live["grouped", "x"] = new_grouped()
-                copy_words(live["bank", "x", half], live["grouped", "x"], half)
+        def copy_value(half):
+            if half == 0:
+                live["grouped", "x"] = new_grouped()
+            copy_words(live["bank", "x", half], live["grouped", "x"], half)
 
         def quantise_value(s):
-            if starts_pair(s):
-                x_codes = pairs.tile([P, N], U32, name="x_codes", align_bytes=64)
-                x_scales = pairs.tile([P, N], U8, name="x_scales", align_bytes=64)
-                quantise(live["grouped", "x"], x_codes, x_scales)
-                live["x_codes", s // H], live["x_scales", s // H] = x_codes, x_scales
+            x_codes = pairs.tile([P, N], U32, name="x_codes", align_bytes=64)
+            x_scales = pairs.tile([P, N], U8, name="x_scales", align_bytes=64)
+            quantise(live["grouped", "x"], x_codes, x_scales)
+            live["x_codes", s // H], live["x_scales", s // H] = x_codes, x_scales
 
         def project_value(s):
             if not is_slice(s):
@@ -187,14 +184,24 @@ def tile_gatedspatialattentionlayer_pb_kernel(
                 )
             live["v_bank", s] = v_bank
 
+        def copy_v(s):
+            if not is_slice(s):
+                return
+            v_words = work.tile([P, HD * PACK], F32, name="v_words")
+            nc.scalar.copy(
+                out=v_words[:].rearrange("p (c i) -> p c i", i=PACK),
+                in_=live["v_bank", s][:].rearrange("p (i c) -> p c i", i=PACK),
+            )
+            live["v_words", s] = v_words
+
         def add_bias(s):
             if not is_slice(s):
                 return
             head = slice((s % H) * HD, (s % H + 1) * HD)
             v_grouped = work.tile([P, HD * PACK], BF16, name="v_grouped", align_bytes=64)
-            nc.vector.tensor_tensor(
+            nc.gpsimd.tensor_tensor(
                 out=v_grouped[:].rearrange("p (c i) -> p c i", i=PACK),
-                in0=live["v_bank", s][:].rearrange("p (i c) -> p c i", i=PACK),
+                in0=live["v_words", s][:].rearrange("p (c i) -> p c i", i=PACK),
                 in1=live["bias"][:, head].unsqueeze(2).to_broadcast([P, HD, PACK]),
                 op=ALU.add,
             )
@@ -230,7 +237,7 @@ def tile_gatedspatialattentionlayer_pb_kernel(
             if not is_slice(s):
                 return
             qkT = work.tile([P, 2 * N], BF16, name="qkT")
-            nc.scalar.copy(out=qkT[:], in_=live["qkT_bank", s][:])
+            nc.scalar.copy(out=qkT[:].bitcast(F32), in_=live["qkT_bank", s][:].bitcast(F32))
             live["qkT", s] = qkT
 
         def score(tile):
@@ -302,18 +309,30 @@ def tile_gatedspatialattentionlayer_pb_kernel(
                     live["grouped", "e", s] = new_grouped()
                 copy_words(live["bank", "e", s, half], live["grouped", "e", s], half)
 
-        def quantise_e(s):
-            if is_slice(s):
-                e_codes = work.tile([P, N], U32, name="e_codes", align_bytes=64)
-                e_scales = work.tile([P, N], U8, name="e_scales", align_bytes=64)
-                quantise(live["grouped", "e", s], e_codes, e_scales)
-                live["e_codes", s], live["e_scales", s] = e_codes, e_scales
+        ALL = range(ROW_TILES)
 
-        def attend(s):
+        def quantise_e(s, tiles=ALL):
             if not is_slice(s):
                 return
-            o_bank = ps_single.tile([P, ROW_TILES * HD], F32, name="o_bank")
-            for j in range(ROW_TILES):
+            if tiles[0] == 0:
+                live["e_codes", s] = work.tile([P, N], U32, name="e_codes", align_bytes=64)
+                live["e_scales", s] = work.tile([P, N], U8, name="e_scales", align_bytes=64)
+            columns = slice(tiles[0] * P, (tiles[-1] + 1) * P)
+            values = slice(tiles[0] * P * PACK, (tiles[-1] + 1) * P * PACK)
+            nc.vector.quantize_mx(
+                out=live["e_codes", s][:, columns].bitcast(FP8X4),
+                scales=live["e_scales", s][:, columns],
+                in_=live["grouped", "e", s][:, values],
+            )
+
+        def attend(s, tiles=ALL):
+            if not is_slice(s):
+                return
+            if s == n_slices - 1:
+                o_bank = ps_score.tile([P, ROW_TILES * HD], F32, name="score")
+            else:
+                o_bank = ps_single.tile([P, ROW_TILES * HD], F32, name="o_bank")
+            for j in tiles:
                 queries = slice(j * P, (j + 1) * P)
                 nc.tensor.matmul_mx(
                     out=o_bank[:, j * HD : (j + 1) * HD],
@@ -324,36 +343,72 @@ def tile_gatedspatialattentionlayer_pb_kernel(
                     start=True,
                     stop=True,
                 )
-            live["o_bank", s] = o_bank
+            live["o_bank", s, tiles[0]] = o_bank
 
-        def invert_sums(s):
+        def invert_sums(s, tiles=ALL):
             if not is_slice(s):
                 return
             inv_sum = work.tile([P, ROW_TILES], F32, name="inv_sum")
-            nc.vector.reciprocal(out=inv_sum[:], in_=live["row_sum", s][:])
-            live["inv_sum", s] = inv_sum
+            columns = slice(tiles[0], tiles[-1] + 1)
+            nc.vector.reciprocal(out=inv_sum[:, columns], in_=live["row_sum", s][:, columns])
+            live["inv_sum", s, tiles[0]] = inv_sum
 
-        def finish(s):
+        def halve_h(s):
+            b, t, h = slices[s]
+            half_h = pairs.tile([P, ROW_TILES * HD], F32, name="half_h")
+            nc.gpsimd.tensor_scalar(
+                out=half_h[:].rearrange("p (j c) -> p j c", j=ROW_TILES),
+                in0=live["h_rows", b, t][:].rearrange("p (j d) -> p j d", j=ROW_TILES)[
+                    :, :, h * HD : (h + 1) * HD
+                ],
+                scalar1=0.5,
+                scalar2=0.0,
+                op0=ALU.mult,
+                op1=ALU.add,
+            )
+            live["half_h", s] = half_h
+
+        def finish(s, tiles=ALL, on_vector=False):
             if not is_slice(s):
                 return
             b, t, h = slices[s]
             head = slice(h * HD, (h + 1) * HD)
             result = work.tile([P, ROW_TILES * HD], F32, name="result")
-            for j in range(ROW_TILES):
+            for j in tiles:
                 nc.scalar.activation(
                     out=result[:, j * HD : (j + 1) * HD],
-                    in_=live["o_bank", s][:, j * HD : (j + 1) * HD],
+                    in_=live["o_bank", s, tiles[0]][:, j * HD : (j + 1) * HD],
                     func=ACT.Tanh,
-                    scale=live["inv_sum", s][:, j : j + 1],
+                    scale=live["inv_sum", s, tiles[0]][:, j : j + 1],
                 )
-            by_tile = result[:].rearrange("p (j c) -> p j c", j=ROW_TILES)
-            other = live["h_rows", b, t][:].rearrange("p (j d) -> p j d", j=ROW_TILES)[:, :, head]
-            nc.gpsimd.tensor_tensor(out=by_tile, in0=by_tile, in1=other, op=ALU.add)
-            nc.gpsimd.tensor_scalar(
-                out=result[:], in0=result[:], scalar1=0.5, scalar2=0.0, op0=ALU.mult, op1=ALU.add
-            )
+            rows = slice(tiles[0], tiles[-1] + 1)
+            columns = slice(tiles[0] * HD, (tiles[-1] + 1) * HD)
+            by_tile = result[:].rearrange("p (j c) -> p j c", j=ROW_TILES)[:, rows]
+            if on_vector:
+                nc.vector.scalar_tensor_tensor(
+                    out=result[:, columns],
+                    in0=result[:, columns],
+                    scalar=0.5,
+                    in1=live["half_h", s][:, columns],
+                    op0=ALU.mult,
+                    op1=ALU.add,
+                )
+            else:
+                other = live["h_rows", b, t][:].rearrange("p (j d) -> p j d", j=ROW_TILES)
+                nc.gpsimd.tensor_tensor(
+                    out=by_tile, in0=by_tile, in1=other[:, rows, head], op=ALU.add
+                )
+                nc.gpsimd.tensor_scalar(
+                    out=result[:, columns],
+                    in0=result[:, columns],
+                    scalar1=0.5,
+                    scalar2=0.0,
+                    op0=ALU.mult,
+                    op1=ALU.add,
+                )
             nc.sync.dma_start(
-                out=out[b, t].rearrange("(p j) d -> p j d", j=ROW_TILES)[:, :, head], in_=by_tile
+                out=out[b, t].rearrange("(p j) d -> p j d", j=ROW_TILES)[:, rows, head],
+                in_=by_tile,
             )
 
         load_q_and_k(0)
@@ -368,30 +423,38 @@ def tile_gatedspatialattentionlayer_pb_kernel(
         load_h(0)
 
         first_step = -ROW_TILES - 2
-        last_step = n_tiles + ROW_TILES + 2
-        for step in range(first_step, last_step + 1):
+        last = n_slices - 1
+        value_step = {}
+        for s in range(0, n_slices, H):
+            value_step[max((s - 1) * ROW_TILES, 0)] = s
+        for step in range(first_step, n_tiles):
             cur, j = divmod(step, ROW_TILES)
 
             if j == 0 and cur >= 0 and is_slice(cur + 3):
                 load_q_and_k(cur + 3)
                 load_gate(cur + 3)
-            if j == 0 and starts_pair(cur + 2) and cur >= 0:
-                load_value(cur + 2)
-                load_h(cur + 2)
+            if j == 0 and starts_pair(cur + 3) and cur >= 0:
+                load_value(cur + 3)
+                load_h(cur + 3)
 
             if j == 0:
                 score(step + 2)
                 attend(cur - 2)
                 score(step + 3)
                 transpose_e(cur - 1, 1)
-                transpose_value(cur, 0)
+            if j == 1 and step == 5:
+                project_value(0)
             if j == 2:
                 score(step + 2)
-                project_value(cur - 1)
+                if cur >= 1:
+                    project_value(cur)
                 score(step + 3)
                 transpose_e(cur, 0)
                 transpose_q_and_k(cur + 2)
-                transpose_value(cur, 1)
+            if step in value_step:
+                transpose_value(value_step[step], 0)
+            if step - 2 in value_step:
+                transpose_value(value_step[step - 2], 1)
             if step == -2:
                 transpose_weights(0)
             if step == 0:
@@ -401,28 +464,57 @@ def tile_gatedspatialattentionlayer_pb_kernel(
                 copy_q_and_k(cur + 1)
             if j == 1:
                 copy_e(cur - 1, 1)
-                copy_value(cur, 0)
             if j == 2:
                 finish(cur - 2)
             if j == 3:
                 copy_e(cur, 0)
-                copy_value(cur, 1)
+                if cur >= 1:
+                    copy_v(cur)
+            if step == 6:
+                copy_v(0)
+            if step - 1 in value_step:
+                copy_value(0)
+            if step - 3 in value_step:
+                copy_value(1)
             if step == -1:
                 copy_weights(0)
             if step == 1:
                 copy_weights(1)
 
+            if step == 6:
+                add_bias(0)
+            if j == 3 and cur >= 1:
+                add_bias(cur)
+            if cur == last - 1 and j == 1:
+                halve_h(last - 1)
+            if cur == last and j == 1:
+                halve_h(last)
+
             gate_scores(step + 1)
             row_max(step)
-            if j == 0:
-                quantise_value(cur - 1)
+            if step - 4 in value_step:
+                quantise_value(value_step[step - 4])
             if j == 2:
                 quantise_e(cur - 1)
-                add_bias(cur - 1)
+                invert_sums(cur - 1)
             if j == 3:
                 quantise_v(cur - 1)
-                invert_sums(cur - 1)
             if step == 3:
                 quantise_weights()
 
             exponentials(step)
+
+        FIRST, SECOND = range(0, 2), range(2, ROW_TILES)
+        attend(last - 1)
+        quantise_e(last, FIRST)
+        quantise_v(last)
+        invert_sums(last, FIRST)
+        transpose_e(last, 1)
+        finish(last - 1, on_vector=True)
+        copy_e(last, 1)
+        attend(last, FIRST)
+        invert_sums(last, SECOND)
+        quantise_e(last, SECOND)
+        finish(last, FIRST, on_vector=True)
+        attend(last, SECOND)
+        finish(last, SECOND, on_vector=True)

@@ -45,6 +45,7 @@ def tile_gatedspatialattentionlayer_pb_kernel(
         loads = stack.enter_context(tc.tile_pool(name="loads", bufs=4))
         pairs = stack.enter_context(tc.tile_pool(name="pairs", bufs=2))
         work = stack.enter_context(tc.tile_pool(name="work", bufs=3))
+        results = stack.enter_context(tc.tile_pool(name="results", bufs=6))
         logits = stack.enter_context(tc.tile_pool(name="logits", bufs=6))
         ps_score = stack.enter_context(tc.psum_pool(name="ps_score", bufs=3))
         ps_words = stack.enter_context(tc.psum_pool(name="ps_words", bufs=2))
@@ -194,14 +195,20 @@ def tile_gatedspatialattentionlayer_pb_kernel(
             )
             live["v_words", s] = v_words
 
+        def bias_on_vector(s):
+            return s % 2 == 1
+
         def add_bias(s):
             if not is_slice(s):
                 return
             head = slice((s % H) * HD, (s % H + 1) * HD)
             v_grouped = work.tile([P, HD * PACK], BF16, name="v_grouped", align_bytes=64)
-            nc.gpsimd.tensor_tensor(
+            engine = nc.vector if bias_on_vector(s) else nc.gpsimd
+            engine.tensor_tensor(
                 out=v_grouped[:].rearrange("p (c i) -> p c i", i=PACK),
-                in0=live["v_words", s][:].rearrange("p (c i) -> p c i", i=PACK),
+                in0=live["v_bank", s][:].rearrange("p (i c) -> p c i", i=PACK)
+                if bias_on_vector(s)
+                else live["v_words", s][:].rearrange("p (c i) -> p c i", i=PACK),
                 in1=live["bias"][:, head].unsqueeze(2).to_broadcast([P, HD, PACK]),
                 op=ALU.add,
             )
@@ -373,7 +380,7 @@ def tile_gatedspatialattentionlayer_pb_kernel(
                 return
             b, t, h = slices[s]
             head = slice(h * HD, (h + 1) * HD)
-            result = work.tile([P, ROW_TILES * HD], F32, name="result")
+            result = results.tile([P, ROW_TILES * HD], F32, name="result")
             for j in tiles:
                 nc.scalar.activation(
                     out=result[:, j * HD : (j + 1) * HD],
@@ -468,7 +475,7 @@ def tile_gatedspatialattentionlayer_pb_kernel(
                 finish(cur - 2)
             if j == 3:
                 copy_e(cur, 0)
-                if cur >= 1:
+                if cur >= 1 and not bias_on_vector(cur):
                     copy_v(cur)
             if step == 6:
                 copy_v(0)
@@ -483,7 +490,7 @@ def tile_gatedspatialattentionlayer_pb_kernel(
 
             if step == 6:
                 add_bias(0)
-            if j == 3 and cur >= 1:
+            if j == 3 and cur >= 1 and not bias_on_vector(cur):
                 add_bias(cur)
             if cur == last - 1 and j == 1:
                 halve_h(last - 1)
@@ -499,6 +506,8 @@ def tile_gatedspatialattentionlayer_pb_kernel(
                 invert_sums(cur - 1)
             if j == 3:
                 quantise_v(cur - 1)
+                if bias_on_vector(cur):
+                    add_bias(cur)
             if step == 3:
                 quantise_weights()
 

@@ -62,6 +62,18 @@ def tile_gatedspatialattentionlayer_pb_kernel(
         one = const.tile([P, 1], F32, name="one")
         nc.scalar.activation(out=one[:], in_=zero[:], func=ACT.Exp)
 
+        zeros = const.tile([P, N // 2], F32, name="zeros")
+        nc.vector.memset(zeros[:], 0.0)
+        for warm_up in range(3):
+            unread = ps_score.tile([P, N], F32, name="score")
+            nc.tensor.matmul(
+                out=unread[:],
+                lhsT=zeros[:].bitcast(BF16)[:, 0:P],
+                rhs=zeros[:].bitcast(BF16),
+                start=True,
+                stop=True,
+            )
+
         def load_q_and_k(s):
             b, t, h = slices[s]
             q_rows = loads.tile([P, ROW_TILES * HD], BF16, name="q_rows")
@@ -79,9 +91,10 @@ def tile_gatedspatialattentionlayer_pb_kernel(
         def load_gate(s):
             b, t, h = slices[s]
             gate = loads.tile([P, ROW_TILES * N], BF16, name="gate")
-            nc.sync.dma_start(
-                out=gate[:], in_=dyn[h * B + b, t].rearrange("(p j) k -> p (j k)", j=ROW_TILES)
-            )
+            rows = dyn[h * B + b, t].rearrange("(p j) k -> p (j k)", j=ROW_TILES)
+            pieces = (slice(0, N), slice(N, ROW_TILES * N)) if s == 0 else (slice(0, ROW_TILES * N),)
+            for columns in pieces:
+                nc.sync.dma_start(out=gate[:, columns], in_=rows[:, columns])
             live["gate", s] = gate
 
         def load_weights():
@@ -114,11 +127,11 @@ def tile_gatedspatialattentionlayer_pb_kernel(
             )
             live["h_rows", b, t] = h_rows
 
-        def transpose_words(rows, half):
+        def transpose_words(rows, tiles):
             words = rows[:].bitcast(F32)
             bank = ps_words.tile([P, BANK], F32, name="wordsT")
-            for part in range(2 * 2):
-                first = 2 * half * WORDS + part * P
+            for part in range(2 * len(tiles)):
+                first = tiles[0] * WORDS + part * P
                 nc.tensor.transpose(
                     out=bank[:, part * P : (part + 1) * P],
                     in_=words[:, first : first + P],
@@ -126,11 +139,12 @@ def tile_gatedspatialattentionlayer_pb_kernel(
                 )
             return bank
 
-        def copy_words(bank, grouped, half):
-            columns = slice(2 * half * P * PACK, 2 * (half + 1) * P * PACK)
-            nc.scalar.copy(
-                out=grouped[:, columns].bitcast(F32).rearrange("p (i r u) -> p i r u", i=2, u=2),
-                in_=bank[:].rearrange("p (i u r) -> p i r u", i=2, u=2),
+        def copy_words(copy, bank, grouped, tiles):
+            i = len(tiles)
+            columns = slice(tiles[0] * P * PACK, (tiles[-1] + 1) * P * PACK)
+            copy(
+                out=grouped[:, columns].bitcast(F32).rearrange("p (i r u) -> p i r u", i=i, u=2),
+                in_=bank[:, : i * WORDS].rearrange("p (i u r) -> p i r u", i=i, u=2),
             )
 
         def new_grouped():
@@ -139,13 +153,15 @@ def tile_gatedspatialattentionlayer_pb_kernel(
         def quantise(grouped, codes, scales):
             nc.vector.quantize_mx(out=codes[:].bitcast(FP8X4), scales=scales[:], in_=grouped[:])
 
+        HALVES = (range(0, 2), range(2, ROW_TILES))
+
         def transpose_weights(half):
-            live["bank", "w", half] = transpose_words(live["rows", "w"], half)
+            live["bank", "w", half] = transpose_words(live["rows", "w"], HALVES[half])
 
         def copy_weights(half):
             if half == 0:
                 live["grouped", "w"] = new_grouped()
-            copy_words(live["bank", "w", half], live["grouped", "w"], half)
+            copy_words(nc.scalar.copy, live["bank", "w", half], live["grouped", "w"], HALVES[half])
 
         def quantise_weights():
             w_codes = const.tile([P, D], U32, name="w_codes", align_bytes=64)
@@ -154,12 +170,12 @@ def tile_gatedspatialattentionlayer_pb_kernel(
             live["w_codes"], live["w_scales"] = w_codes, w_scales
 
         def transpose_value(s, half):
-            live["bank", "x", half] = transpose_words(live["rows", "x", s], half)
+            live["bank", "x", half] = transpose_words(live["rows", "x", s], HALVES[half])
 
         def copy_value(half):
             if half == 0:
                 live["grouped", "x"] = new_grouped()
-            copy_words(live["bank", "x", half], live["grouped", "x"], half)
+            copy_words(nc.scalar.copy, live["bank", "x", half], live["grouped", "x"], HALVES[half])
 
         def quantise_value(s):
             x_codes = pairs.tile([P, N], U32, name="x_codes", align_bytes=64)
@@ -196,7 +212,7 @@ def tile_gatedspatialattentionlayer_pb_kernel(
             live["v_words", s] = v_words
 
         def bias_on_vector(s):
-            return s % 2 == 1
+            return s % 2 == 1 or s == 0
 
         def add_bias(s):
             if not is_slice(s):
@@ -290,31 +306,36 @@ def tile_gatedspatialattentionlayer_pb_kernel(
                 negate=True,
             )
 
+        def sum_column(s, j):
+            column = s % 2 * ROW_TILES + j
+            return slice(column, column + 1)
+
         def exponentials(tile):
             if not 0 <= tile < n_tiles:
                 return
             s, j = divmod(tile, ROW_TILES)
             if j == 0:
                 live["rows", "e", s] = work.tile([P, ROW_TILES * N], BF16, name="e_rows")
-                live["row_sum", s] = work.tile([P, ROW_TILES], F32, name="row_sum")
+                if s % 2 == 0:
+                    live["row_sum", s // 2] = work.tile([P, 2 * ROW_TILES], F32, name="row_sum")
             nc.scalar.activation(
                 out=live["rows", "e", s][:, j * N : (j + 1) * N],
                 in_=live["g", tile][:],
                 func=ACT.Exp,
                 bias=live["neg_max", s][:, j : j + 1],
                 scale=1.0,
-                accum_out=live["row_sum", s][:, j : j + 1],
+                accum_out=live["row_sum", s // 2][:, sum_column(s, j)],
             )
 
-        def transpose_e(s, half):
+        def transpose_e(s, tiles):
             if is_slice(s):
-                live["bank", "e", s, half] = transpose_words(live["rows", "e", s], half)
+                live["bank", "e", s, tiles[0]] = transpose_words(live["rows", "e", s], tiles)
 
-        def copy_e(s, half):
+        def copy_e(s, tiles, copy=nc.scalar.copy):
             if is_slice(s):
-                if half == 0:
+                if tiles[0] == 0:
                     live["grouped", "e", s] = new_grouped()
-                copy_words(live["bank", "e", s, half], live["grouped", "e", s], half)
+                copy_words(copy, live["bank", "e", s, tiles[0]], live["grouped", "e", s], tiles)
 
         ALL = range(ROW_TILES)
 
@@ -352,13 +373,12 @@ def tile_gatedspatialattentionlayer_pb_kernel(
                 )
             live["o_bank", s, tiles[0]] = o_bank
 
-        def invert_sums(s, tiles=ALL):
-            if not is_slice(s):
-                return
-            inv_sum = work.tile([P, ROW_TILES], F32, name="inv_sum")
-            columns = slice(tiles[0], tiles[-1] + 1)
-            nc.vector.reciprocal(out=inv_sum[:, columns], in_=live["row_sum", s][:, columns])
-            live["inv_sum", s, tiles[0]] = inv_sum
+        def invert_sums(two, columns=slice(0, 2 * ROW_TILES)):
+            if columns.start == 0:
+                live["inv_sum", two] = work.tile([P, 2 * ROW_TILES], F32, name="inv_sum")
+            nc.vector.reciprocal(
+                out=live["inv_sum", two][:, columns], in_=live["row_sum", two][:, columns]
+            )
 
         def halve_h(s):
             b, t, h = slices[s]
@@ -375,48 +395,57 @@ def tile_gatedspatialattentionlayer_pb_kernel(
             )
             live["half_h", s] = half_h
 
-        def finish(s, tiles=ALL, on_vector=False):
-            if not is_slice(s):
-                return
-            b, t, h = slices[s]
-            head = slice(h * HD, (h + 1) * HD)
+        def tanh_of_mean(s, tiles=ALL):
             result = results.tile([P, ROW_TILES * HD], F32, name="result")
             for j in tiles:
                 nc.scalar.activation(
                     out=result[:, j * HD : (j + 1) * HD],
                     in_=live["o_bank", s, tiles[0]][:, j * HD : (j + 1) * HD],
                     func=ACT.Tanh,
-                    scale=live["inv_sum", s, tiles[0]][:, j : j + 1],
+                    scale=live["inv_sum", s // 2][:, sum_column(s, j)],
                 )
+            live["result", s, tiles[0]] = result
+
+        def store(s, tiles=ALL):
+            b, t, h = slices[s]
             rows = slice(tiles[0], tiles[-1] + 1)
-            columns = slice(tiles[0] * HD, (tiles[-1] + 1) * HD)
-            by_tile = result[:].rearrange("p (j c) -> p j c", j=ROW_TILES)[:, rows]
-            if on_vector:
-                nc.vector.scalar_tensor_tensor(
-                    out=result[:, columns],
-                    in0=result[:, columns],
-                    scalar=0.5,
-                    in1=live["half_h", s][:, columns],
-                    op0=ALU.mult,
-                    op1=ALU.add,
-                )
-            else:
-                other = live["h_rows", b, t][:].rearrange("p (j d) -> p j d", j=ROW_TILES)
-                nc.gpsimd.tensor_tensor(
-                    out=by_tile, in0=by_tile, in1=other[:, rows, head], op=ALU.add
-                )
-                nc.gpsimd.tensor_scalar(
-                    out=result[:, columns],
-                    in0=result[:, columns],
-                    scalar1=0.5,
-                    scalar2=0.0,
-                    op0=ALU.mult,
-                    op1=ALU.add,
-                )
+            by_tile = live["result", s, tiles[0]][:].rearrange("p (j c) -> p j c", j=ROW_TILES)
             nc.sync.dma_start(
-                out=out[b, t].rearrange("(p j) d -> p j d", j=ROW_TILES)[:, rows, head],
-                in_=by_tile,
+                out=out[b, t].rearrange("(p j) d -> p j d", j=ROW_TILES)[
+                    :, rows, h * HD : (h + 1) * HD
+                ],
+                in_=by_tile[:, rows],
             )
+
+        def average_on_gpsimd(s):
+            b, t, h = slices[s]
+            result = live["result", s, 0]
+            by_tile = result[:].rearrange("p (j c) -> p j c", j=ROW_TILES)
+            other = live["h_rows", b, t][:].rearrange("p (j d) -> p j d", j=ROW_TILES)
+            nc.gpsimd.tensor_tensor(
+                out=by_tile, in0=by_tile, in1=other[:, :, h * HD : (h + 1) * HD], op=ALU.add
+            )
+            nc.gpsimd.tensor_scalar(
+                out=result[:], in0=result[:], scalar1=0.5, scalar2=0.0, op0=ALU.mult, op1=ALU.add
+            )
+
+        def average_on_vector(s, tiles=ALL):
+            columns = slice(tiles[0] * HD, (tiles[-1] + 1) * HD)
+            result = live["result", s, tiles[0]]
+            nc.vector.scalar_tensor_tensor(
+                out=result[:, columns],
+                in0=result[:, columns],
+                scalar=0.5,
+                in1=live["half_h", s][:, columns],
+                op0=ALU.mult,
+                op1=ALU.add,
+            )
+
+        def finish(s):
+            if is_slice(s):
+                tanh_of_mean(s)
+                average_on_gpsimd(s)
+                store(s)
 
         load_q_and_k(0)
         load_gate(0)
@@ -428,8 +457,14 @@ def tile_gatedspatialattentionlayer_pb_kernel(
         load_q_and_k(2)
         load_gate(2)
         load_h(0)
+        transpose_q_and_k(0)
+        copy_q_and_k(0)
+        score(0)
+        score(1)
+        transpose_q_and_k(1)
+        transpose_weights(0)
 
-        first_step = -ROW_TILES - 2
+        first_step = -1
         last = n_slices - 1
         value_step = {}
         for s in range(0, n_slices, H):
@@ -448,7 +483,7 @@ def tile_gatedspatialattentionlayer_pb_kernel(
                 score(step + 2)
                 attend(cur - 2)
                 score(step + 3)
-                transpose_e(cur - 1, 1)
+                transpose_e(cur - 1, HALVES[1])
             if j == 1 and step == 5:
                 project_value(0)
             if j == 2:
@@ -456,29 +491,25 @@ def tile_gatedspatialattentionlayer_pb_kernel(
                 if cur >= 1:
                     project_value(cur)
                 score(step + 3)
-                transpose_e(cur, 0)
+                transpose_e(cur, HALVES[0])
                 transpose_q_and_k(cur + 2)
             if step in value_step:
                 transpose_value(value_step[step], 0)
             if step - 2 in value_step:
                 transpose_value(value_step[step - 2], 1)
-            if step == -2:
-                transpose_weights(0)
             if step == 0:
                 transpose_weights(1)
 
             if j == 0:
                 copy_q_and_k(cur + 1)
             if j == 1:
-                copy_e(cur - 1, 1)
+                copy_e(cur - 1, HALVES[1])
             if j == 2:
                 finish(cur - 2)
             if j == 3:
-                copy_e(cur, 0)
+                copy_e(cur, HALVES[0])
                 if cur >= 1 and not bias_on_vector(cur):
                     copy_v(cur)
-            if step == 6:
-                copy_v(0)
             if step - 1 in value_step:
                 copy_value(0)
             if step - 3 in value_step:
@@ -488,8 +519,6 @@ def tile_gatedspatialattentionlayer_pb_kernel(
             if step == 1:
                 copy_weights(1)
 
-            if step == 6:
-                add_bias(0)
             if j == 3 and cur >= 1 and not bias_on_vector(cur):
                 add_bias(cur)
             if cur == last - 1 and j == 1:
@@ -501,29 +530,41 @@ def tile_gatedspatialattentionlayer_pb_kernel(
             row_max(step)
             if step - 4 in value_step:
                 quantise_value(value_step[step - 4])
+            if step == 5:
+                add_bias(0)
             if j == 2:
                 quantise_e(cur - 1)
-                invert_sums(cur - 1)
-            if j == 3:
                 quantise_v(cur - 1)
-                if bias_on_vector(cur):
-                    add_bias(cur)
+            if j == 1 and cur >= 2 and cur % 2 == 0:
+                invert_sums(cur // 2 - 1)
+            if j == 3 and cur >= 1 and bias_on_vector(cur):
+                add_bias(cur)
             if step == 3:
                 quantise_weights()
 
             exponentials(step)
 
-        FIRST, SECOND = range(0, 2), range(2, ROW_TILES)
+        first = HALVES[0]
         attend(last - 1)
-        quantise_e(last, FIRST)
+        quantise_e(last, first)
         quantise_v(last)
-        invert_sums(last, FIRST)
-        transpose_e(last, 1)
-        finish(last - 1, on_vector=True)
-        copy_e(last, 1)
-        attend(last, FIRST)
-        invert_sums(last, SECOND)
-        quantise_e(last, SECOND)
-        finish(last, FIRST, on_vector=True)
-        attend(last, SECOND)
-        finish(last, SECOND, on_vector=True)
+        invert_sums(last // 2, slice(0, 6))
+        tanh_of_mean(last - 1)
+        transpose_e(last, [2])
+        transpose_e(last, [3])
+        attend(last, first)
+        tanh_of_mean(last, first)
+        copy_e(last, [2], nc.vector.tensor_copy)
+        copy_e(last, [3], nc.vector.tensor_copy)
+        quantise_e(last, [2])
+        invert_sums(last // 2, slice(6, 8))
+        quantise_e(last, [3])
+        average_on_vector(last - 1)
+        store(last - 1)
+        average_on_vector(last, first)
+        store(last, first)
+        for tiles in [2], [3]:
+            attend(last, tiles)
+            tanh_of_mean(last, tiles)
+            average_on_vector(last, tiles)
+            store(last, tiles)

@@ -212,7 +212,7 @@ def tile_gatedspatialattentionlayer_pb_kernel(
             live["v_words", s] = v_words
 
         def bias_on_vector(s):
-            return s % 2 == 1 or s == 0
+            return s == 0
 
         def add_bias(s):
             if not is_slice(s):
@@ -480,6 +480,8 @@ def tile_gatedspatialattentionlayer_pb_kernel(
                 load_h(cur + 3)
 
             if j == 0:
+                if cur == last:
+                    project_value(last)
                 score(step + 2)
                 attend(cur - 2)
                 score(step + 3)
@@ -488,7 +490,7 @@ def tile_gatedspatialattentionlayer_pb_kernel(
                 project_value(0)
             if j == 2:
                 score(step + 2)
-                if cur >= 1:
+                if 1 <= cur < last:
                     project_value(cur)
                 score(step + 3)
                 transpose_e(cur, HALVES[0])
@@ -507,9 +509,11 @@ def tile_gatedspatialattentionlayer_pb_kernel(
             if j == 2:
                 finish(cur - 2)
             if j == 3:
-                copy_e(cur, HALVES[0])
-                if cur >= 1 and not bias_on_vector(cur):
+                if 1 <= cur < last:
                     copy_v(cur)
+                copy_e(cur, HALVES[0])
+            if j == 0 and cur == last:
+                copy_v(last)
             if step - 1 in value_step:
                 copy_value(0)
             if step - 3 in value_step:
@@ -519,17 +523,17 @@ def tile_gatedspatialattentionlayer_pb_kernel(
             if step == 1:
                 copy_weights(1)
 
-            if j == 3 and cur >= 1 and not bias_on_vector(cur):
+            if j == 3 and 1 <= cur < last or j == 0 and cur == last:
                 add_bias(cur)
-            if cur == last - 1 and j == 1:
-                halve_h(last - 1)
-            if cur == last and j == 1:
-                halve_h(last)
+            if j == 1 and cur in (last - 3, last - 2):
+                halve_h(cur + 2)
 
             gate_scores(step + 1)
             row_max(step)
-            if step - 4 in value_step:
-                quantise_value(value_step[step - 4])
+            if step == 4:
+                quantise_value(0)
+            if j == 1 and starts_pair(cur) and cur > 0:
+                quantise_value(cur)
             if step == 5:
                 add_bias(0)
             if j == 2:
@@ -537,8 +541,8 @@ def tile_gatedspatialattentionlayer_pb_kernel(
                 quantise_v(cur - 1)
             if j == 1 and cur >= 2 and cur % 2 == 0:
                 invert_sums(cur // 2 - 1)
-            if j == 3 and cur >= 1 and bias_on_vector(cur):
-                add_bias(cur)
+            if j == 1 and cur == last:
+                invert_sums(last // 2, slice(0, 4))
             if step == 3:
                 quantise_weights()
 
@@ -546,17 +550,17 @@ def tile_gatedspatialattentionlayer_pb_kernel(
 
         first = HALVES[0]
         attend(last - 1)
-        quantise_e(last, first)
-        quantise_v(last)
-        invert_sums(last // 2, slice(0, 6))
         tanh_of_mean(last - 1)
         transpose_e(last, [2])
         transpose_e(last, [3])
+        copy_e(last, [2], nc.vector.tensor_copy)
+        quantise_e(last, first)
+        quantise_v(last)
+        quantise_e(last, [2])
+        invert_sums(last // 2, slice(4, 6))
         attend(last, first)
         tanh_of_mean(last, first)
-        copy_e(last, [2], nc.vector.tensor_copy)
         copy_e(last, [3], nc.vector.tensor_copy)
-        quantise_e(last, [2])
         invert_sums(last // 2, slice(6, 8))
         quantise_e(last, [3])
         average_on_vector(last - 1)

@@ -106,8 +106,20 @@ def tile_gatedspatialattentionlayer_pb_kernel(
             live["rows", "w"] = w_rows
 
         def load_bias():
-            bias = const.tile([P, D], BF16, name="bias")
-            nc.sync.dma_start(out=bias[:], in_=bv.partition_broadcast(P))
+            bias_row = const.tile([P, D], BF16, name="bias_row")
+            nc.vector.memset(bias_row[:], 0.0)
+            nc.sync.dma_start(out=bias_row[0:1, :], in_=bv.rearrange("(o d) -> o d", o=1))
+            live["bias_row"] = bias_row
+
+        def spread_bias():
+            ones = const.tile([P, P], BF16, name="ones")
+            nc.vector.memset(ones[:], 1.0)
+            bank = ps_words.tile([P, BANK], F32, name="wordsT")
+            nc.tensor.matmul(
+                out=bank[:], lhsT=ones[:], rhs=live["bias_row"][:], start=True, stop=True
+            )
+            bias = const.tile([P, D], F32, name="bias")
+            nc.scalar.copy(out=bias[:], in_=bank[:])
             live["bias"] = bias
 
         def load_value(s):
@@ -448,11 +460,11 @@ def tile_gatedspatialattentionlayer_pb_kernel(
                 store(s)
 
         load_q_and_k(0)
-        load_gate(0)
-        load_q_and_k(1)
-        load_weights()
-        load_value(0)
         load_bias()
+        load_gate(0)
+        load_weights()
+        load_q_and_k(1)
+        load_value(0)
         load_gate(1)
         load_q_and_k(2)
         load_gate(2)
@@ -461,7 +473,7 @@ def tile_gatedspatialattentionlayer_pb_kernel(
         copy_q_and_k(0)
         score(0)
         score(1)
-        transpose_q_and_k(1)
+        spread_bias()
         transpose_weights(0)
 
         first_step = -1
@@ -479,6 +491,9 @@ def tile_gatedspatialattentionlayer_pb_kernel(
                 load_value(cur + 3)
                 load_h(cur + 3)
 
+            if j == 2 and starts_pair(cur) and cur > 0:
+                quantise_value(cur)
+
             if j == 0:
                 if cur == last:
                     project_value(last)
@@ -495,6 +510,8 @@ def tile_gatedspatialattentionlayer_pb_kernel(
                 score(step + 3)
                 transpose_e(cur, HALVES[0])
                 transpose_q_and_k(cur + 2)
+            if step == 0:
+                transpose_q_and_k(1)
             if step in value_step:
                 transpose_value(value_step[step], 0)
             if step - 2 in value_step:
@@ -502,7 +519,7 @@ def tile_gatedspatialattentionlayer_pb_kernel(
             if step == 0:
                 transpose_weights(1)
 
-            if j == 0:
+            if j == 0 and cur > 0 or step == 1:
                 copy_q_and_k(cur + 1)
             if j == 1:
                 copy_e(cur - 1, HALVES[1])
@@ -532,8 +549,6 @@ def tile_gatedspatialattentionlayer_pb_kernel(
             row_max(step)
             if step == 4:
                 quantise_value(0)
-            if j == 1 and starts_pair(cur) and cur > 0:
-                quantise_value(cur)
             if step == 5:
                 add_bias(0)
             if j == 2:

import math
from contextlib import ExitStack

import concourse.mybir as mybir
from concourse.masks import make_identity

BF16 = mybir.dt.bfloat16
F32 = mybir.dt.float32
U32 = mybir.dt.uint32
U8 = mybir.dt.uint8
FP8X4 = mybir.dt.float8_e4m3fn_x4
ALU = mybir.AluOpType
ACT = mybir.ActivationFunctionType
AXIS = mybir.AxisListType

P = 128
B, T, N, D, H = 2, 2, 512, 512, 4
HD = D // H
ROW_TILES = N // P
PACK = 4
K = 512
WORDS = K // 2
BANK = 512

FLOPS = 2 * B * T * N * D * D + 2 * (2 * H * B * T * N * N * HD)


def tile_gatedspatialattentionlayer_pb_kernel(
    tc, q_heads, k_heads, value, Wv, bv, dyn, h_gcn, out
):
    nc = tc.nc
    slices = [(b, t, h) for b in range(B) for t in range(T) for h in range(H)]
    n_slices = len(slices)
    n_tiles = n_slices * ROW_TILES
    live = {}

    def is_slice(s):
        return 0 <= s < n_slices

    def starts_pair(s):
        return is_slice(s) and s % H == 0

    with ExitStack() as stack:
        const = stack.enter_context(tc.tile_pool(name="const", bufs=1))
        loads = stack.enter_context(tc.tile_pool(name="loads", bufs=4))
        pairs = stack.enter_context(tc.tile_pool(name="pairs", bufs=2))
        work = stack.enter_context(tc.tile_pool(name="work", bufs=3))
        results = stack.enter_context(tc.tile_pool(name="results", bufs=6))
        logits = stack.enter_context(tc.tile_pool(name="logits", bufs=6))
        ps_score = stack.enter_context(tc.psum_pool(name="ps_score", bufs=3))
        ps_words = stack.enter_context(tc.psum_pool(name="ps_words", bufs=2))
        ps_single = stack.enter_context(tc.psum_pool(name="ps_single", bufs=1))
        stack.enter_context(tc.manual_schedule())

        ident_bf16 = const.tile([P, P], BF16, name="ident_bf16")
        make_identity(nc, ident_bf16[:])
        ident_f32 = const.tile([P, P], F32, name="ident_f32")
        make_identity(nc, ident_f32[:])

        zero = const.tile([P, 1], F32, name="zero")
        nc.vector.memset(zero[:], 0.0)
        one = const.tile([P, 1], F32, name="one")
        nc.scalar.activation(out=one[:], in_=zero[:], func=ACT.Exp)

        zeros = const.tile([P, N // 2], F32, name="zeros")
        nc.vector.memset(zeros[:], 0.0)
        for warm_up in range(3):
            unread = ps_score.tile([P, N], F32, name="score")
            nc.tensor.matmul(
                out=unread[:],
                lhsT=zeros[:].bitcast(BF16)[:, 0:P],
                rhs=zeros[:].bitcast(BF16),
                start=True,
                stop=True,
            )

        def load_q_and_k(s):
            b, t, h = slices[s]
            q_rows = loads.tile([P, ROW_TILES * HD], BF16, name="q_rows")
            nc.sync.dma_start(
                out=q_rows[:],
                in_=q_heads[h * B + b, t].rearrange("(p j) d -> p (j d)", j=ROW_TILES),
            )
            k_rows = loads.tile([P, ROW_TILES * HD], BF16, name="k_rows")
            nc.sync.dma_start(
                out=k_rows[:].rearrange("p (j d) -> p j d", j=ROW_TILES),
                in_=k_heads[h * B + b, t].rearrange("(j p) d -> p j d", p=P),
            )
            live["q_rows", s], live["k_rows", s] = q_rows, k_rows

        def load_gate(s):
            b, t, h = slices[s]
            gate = loads.tile([P, ROW_TILES * N], BF16, name="gate")
            rows = dyn[h * B + b, t].rearrange("(p j) k -> p (j k)", j=ROW_TILES)
            pieces = (slice(0, N), slice(N, ROW_TILES * N)) if s == 0 else (slice(0, ROW_TILES * N),)
            for columns in pieces:
                nc.sync.dma_start(out=gate[:, columns], in_=rows[:, columns])
            live["gate", s] = gate

        def load_weights():
            w_rows = pairs.tile([P, ROW_TILES * K], BF16, name="rows")
            nc.sync.dma_start(
                out=w_rows[:].rearrange("p (i k) -> p i k", i=ROW_TILES),
                in_=Wv.rearrange("(i p) k -> p i k", p=P),
            )
            live["rows", "w"] = w_rows

        def load_bias():
            bias_row = const.tile([P, D], BF16, name="bias_row")
            nc.vector.memset(bias_row[:], 0.0)
            nc.sync.dma_start(out=bias_row[0:1, :], in_=bv.rearrange("(o d) -> o d", o=1))
            live["bias_row"] = bias_row

        def spread_bias():
            ones = const.tile([P, P], BF16, name="ones")
            nc.vector.memset(ones[:], 1.0)
            bank = ps_words.tile([P, BANK], F32, name="wordsT")
            nc.tensor.matmul(
                out=bank[:], lhsT=ones[:], rhs=live["bias_row"][:], start=True, stop=True
            )
            bias = const.tile([P, D], F32, name="bias")
            nc.scalar.copy(out=bias[:], in_=bank[:])
            live["bias"] = bias

        def load_value(s):
            b, t, h = slices[s]
            v_rows = pairs.tile([P, ROW_TILES * K], BF16, name="rows")
            nc.sync.dma_start(
                out=v_rows[:].rearrange("p (u x) -> p u x", u=2),
                in_=value[b, t].rearrange("(u p e) d -> p u (e d)", u=2, e=2),
            )
            live["rows", "x", s] = v_rows

        def load_h(s):
            b, t, h = slices[s]
            h_rows = pairs.tile([P, ROW_TILES * D], BF16, name="h_rows")
            nc.sync.dma_start(
                out=h_rows[:], in_=h_gcn[b, t].rearrange("(p j) d -> p (j d)", j=ROW_TILES)
            )
            live["h_rows", b, t] = h_rows

        def transpose_words(rows, tiles):
            words = rows[:].bitcast(F32)
            bank = ps_words.tile([P, BANK], F32, name="wordsT")
            for part in range(2 * len(tiles)):
                first = tiles[0] * WORDS + part * P
                nc.tensor.transpose(
                    out=bank[:, part * P : (part + 1) * P],
                    in_=words[:, first : first + P],
                    identity=ident_f32[:],
                )
            return bank

        def copy_words(copy, bank, grouped, tiles):
            i = len(tiles)
            columns = slice(tiles[0] * P * PACK, (tiles[-1] + 1) * P * PACK)
            copy(
                out=grouped[:, columns].bitcast(F32).rearrange("p (i r u) -> p i r u", i=i, u=2),
                in_=bank[:, : i * WORDS].rearrange("p (i u r) -> p i r u", i=i, u=2),
            )

        def new_grouped():
            return work.tile([P, ROW_TILES * P * PACK], BF16, name="grouped", align_bytes=64)

        def quantise(grouped, codes, scales):
            nc.vector.quantize_mx(out=codes[:].bitcast(FP8X4), scales=scales[:], in_=grouped[:])

        HALVES = (range(0, 2), range(2, ROW_TILES))

        def transpose_weights(half):
            live["bank", "w", half] = transpose_words(live["rows", "w"], HALVES[half])

        def copy_weights(half):
            if half == 0:
                live["grouped", "w"] = new_grouped()
            copy_words(nc.scalar.copy, live["bank", "w", half], live["grouped", "w"], HALVES[half])

        def quantise_weights():
            w_codes = const.tile([P, D], U32, name="w_codes", align_bytes=64)
            w_scales = const.tile([P, D], U8, name="w_scales", align_bytes=64)
            quantise(live["grouped", "w"], w_codes, w_scales)
            live["w_codes"], live["w_scales"] = w_codes, w_scales

        def transpose_value(s, half):
            live["bank", "x", half] = transpose_words(live["rows", "x", s], HALVES[half])

        def copy_value(half):
            if half == 0:
                live["grouped", "x"] = new_grouped()
            copy_words(nc.scalar.copy, live["bank", "x", half], live["grouped", "x"], HALVES[half])

        def quantise_value(s):
            x_codes = pairs.tile([P, N], U32, name="x_codes", align_bytes=64)
            x_scales = pairs.tile([P, N], U8, name="x_scales", align_bytes=64)
            quantise(live["grouped", "x"], x_codes, x_scales)
            live["x_codes", s // H], live["x_scales", s // H] = x_codes, x_scales

        def project_value(s):
            if not is_slice(s):
                return
            head = slice((s % H) * HD, (s % H + 1) * HD)
            v_bank = ps_single.tile([P, PACK * HD], F32, name="v_bank")
            for i in range(PACK):
                nodes = slice(i * P, (i + 1) * P)
                nc.tensor.matmul_mx(
                    out=v_bank[:, i * HD : (i + 1) * HD],
                    lhsT=live["x_codes", s // H][:, nodes].bitcast(FP8X4),
                    lhsT_scale=live["x_scales", s // H][:, nodes],
                    rhs=live["w_codes"][:, head].bitcast(FP8X4),
                    rhs_scale=live["w_scales"][:, head],
                    start=True,
                    stop=True,
                )
            live["v_bank", s] = v_bank

        def copy_v(s):
            if not is_slice(s):
                return
            v_words = work.tile([P, HD * PACK], F32, name="v_words")
            nc.scalar.copy(
                out=v_words[:].rearrange("p (c i) -> p c i", i=PACK),
                in_=live["v_bank", s][:].rearrange("p (i c) -> p c i", i=PACK),
            )
            live["v_words", s] = v_words

        def bias_on_vector(s):
            return s == 0

        def add_bias(s):
            if not is_slice(s):
                return
            head = slice((s % H) * HD, (s % H + 1) * HD)
            v_grouped = work.tile([P, HD * PACK], BF16, name="v_grouped", align_bytes=64)
            engine = nc.vector if bias_on_vector(s) else nc.gpsimd
            engine.tensor_tensor(
                out=v_grouped[:].rearrange("p (c i) -> p c i", i=PACK),
                in0=live["v_bank", s][:].rearrange("p (i c) -> p c i", i=PACK)
                if bias_on_vector(s)
                else live["v_words", s][:].rearrange("p (c i) -> p c i", i=PACK),
                in1=live["bias"][:, head].unsqueeze(2).to_broadcast([P, HD, PACK]),
                op=ALU.add,
            )
            live["v_grouped", s] = v_grouped

        def quantise_v(s):
            if not is_slice(s):
                return
            v_codes = work.tile([P, HD], U32, name="v_codes", align_bytes=64)
            v_scales = work.tile([P, HD], U8, name="v_scales", align_bytes=64)
            quantise(live["v_grouped", s], v_codes, v_scales)
            live["v_codes", s], live["v_scales", s] = v_codes, v_scales

        def transpose_q_and_k(s):
            if not is_slice(s):
                return
            qkT_bank = ps_single.tile([P, 2 * N], BF16, name="qkT_bank")
            for j in range(ROW_TILES):
                nc.tensor.transpose(
                    out=qkT_bank[:, j * P : (j + 1) * P],
                    in_=live["q_rows", s][:, j * HD : (j + 1) * HD],
                    identity=ident_bf16[:],
                )
            for j in range(ROW_TILES):
                nc.tensor.transpose(
                    out=qkT_bank[:, N + j * P : N + (j + 1) * P],
                    in_=live["k_rows", s][:, j * HD : (j + 1) * HD],
                    identity=ident_bf16[:],
                )
            live["qkT_bank", s] = qkT_bank

        def copy_q_and_k(s):
            if not is_slice(s):
                return
            qkT = work.tile([P, 2 * N], BF16, name="qkT")
            nc.scalar.copy(out=qkT[:].bitcast(F32), in_=live["qkT_bank", s][:].bitcast(F32))
            live["qkT", s] = qkT

        def score(tile):
            if not 0 <= tile < n_tiles:
                return
            s, j = divmod(tile, ROW_TILES)
            bank = ps_score.tile([P, N], F32, name="score")
            nc.tensor.matmul(
                out=bank[:],
                lhsT=live["qkT", s][:, j * P : (j + 1) * P],
                rhs=live["qkT", s][:, N : 2 * N],
                start=True,
                stop=True,
            )
            live["score", tile] = bank

        def gate_scores(tile):
            if not 0 <= tile < n_tiles:
                return
            s, j = divmod(tile, ROW_TILES)
            g = logits.tile([P, N], F32, name="g")
            nc.vector.scalar_tensor_tensor(
                out=g[:],
                in0=live["score", tile][:],
                scalar=1.0 / math.sqrt(HD),
                in1=live["gate", s][:, j * N : (j + 1) * N],
                op0=ALU.mult,
                op1=ALU.mult,
            )
            live["g", tile] = g

        def row_max(tile):
            if not 0 <= tile < n_tiles:
                return
            s, j = divmod(tile, ROW_TILES)
            if j == 0:
                live["neg_max", s] = work.tile([P, ROW_TILES], F32, name="neg_max")
            nc.vector.tensor_reduce(
                out=live["neg_max", s][:, j : j + 1],
                in_=live["g", tile][:],
                axis=AXIS.X,
                op=ALU.max,
                negate=True,
            )

        def sum_column(s, j):
            column = s % 2 * ROW_TILES + j
            return slice(column, column + 1)

        def exponentials(tile):
            if not 0 <= tile < n_tiles:
                return
            s, j = divmod(tile, ROW_TILES)
            if j == 0:
                live["rows", "e", s] = work.tile([P, ROW_TILES * N], BF16, name="e_rows")
                if s % 2 == 0:
                    live["row_sum", s // 2] = work.tile([P, 2 * ROW_TILES], F32, name="row_sum")
            nc.scalar.activation(
                out=live["rows", "e", s][:, j * N : (j + 1) * N],
                in_=live["g", tile][:],
                func=ACT.Exp,
                bias=live["neg_max", s][:, j : j + 1],
                scale=1.0,
                accum_out=live["row_sum", s // 2][:, sum_column(s, j)],
            )

        def transpose_e(s, tiles):
            if is_slice(s):
                live["bank", "e", s, tiles[0]] = transpose_words(live["rows", "e", s], tiles)

        def copy_e(s, tiles, copy=nc.scalar.copy):
            if is_slice(s):
                if tiles[0] == 0:
                    live["grouped", "e", s] = new_grouped()
                copy_words(copy, live["bank", "e", s, tiles[0]], live["grouped", "e", s], tiles)

        ALL = range(ROW_TILES)

        def quantise_e(s, tiles=ALL):
            if not is_slice(s):
                return
            if tiles[0] == 0:
                live["e_codes", s] = work.tile([P, N], U32, name="e_codes", align_bytes=64)
                live["e_scales", s] = work.tile([P, N], U8, name="e_scales", align_bytes=64)
            columns = slice(tiles[0] * P, (tiles[-1] + 1) * P)
            values = slice(tiles[0] * P * PACK, (tiles[-1] + 1) * P * PACK)
            nc.vector.quantize_mx(
                out=live["e_codes", s][:, columns].bitcast(FP8X4),
                scales=live["e_scales", s][:, columns],
                in_=live["grouped", "e", s][:, values],
            )

        def attend(s, tiles=ALL):
            if not is_slice(s):
                return
            if s == n_slices - 1:
                o_bank = ps_score.tile([P, ROW_TILES * HD], F32, name="score")
            else:
                o_bank = ps_single.tile([P, ROW_TILES * HD], F32, name="o_bank")
            for j in tiles:
                queries = slice(j * P, (j + 1) * P)
                nc.tensor.matmul_mx(
                    out=o_bank[:, j * HD : (j + 1) * HD],
                    lhsT=live["e_codes", s][:, queries].bitcast(FP8X4),
                    lhsT_scale=live["e_scales", s][:, queries],
                    rhs=live["v_codes", s][:].bitcast(FP8X4),
                    rhs_scale=live["v_scales", s][:],
                    start=True,
                    stop=True,
                )
            live["o_bank", s, tiles[0]] = o_bank

        def invert_sums(two, columns=slice(0, 2 * ROW_TILES)):
            if columns.start == 0:
                live["inv_sum", two] = work.tile([P, 2 * ROW_TILES], F32, name="inv_sum")
            nc.vector.reciprocal(
                out=live["inv_sum", two][:, columns], in_=live["row_sum", two][:, columns]
            )

        def halve_h(s):
            b, t, h = slices[s]
            half_h = pairs.tile([P, ROW_TILES * HD], F32, name="half_h")
            nc.gpsimd.tensor_scalar(
                out=half_h[:].rearrange("p (j c) -> p j c", j=ROW_TILES),
                in0=live["h_rows", b, t][:].rearrange("p (j d) -> p j d", j=ROW_TILES)[
                    :, :, h * HD : (h + 1) * HD
                ],
                scalar1=0.5,
                scalar2=0.0,
                op0=ALU.mult,
                op1=ALU.add,
            )
            live["half_h", s] = half_h

        def tanh_of_mean(s, tiles=ALL):
            result = results.tile([P, ROW_TILES * HD], F32, name="result")
            for j in tiles:
                nc.scalar.activation(
                    out=result[:, j * HD : (j + 1) * HD],
                    in_=live["o_bank", s, tiles[0]][:, j * HD : (j + 1) * HD],
                    func=ACT.Tanh,
                    scale=live["inv_sum", s // 2][:, sum_column(s, j)],
                )
            live["result", s, tiles[0]] = result

        def store(s, tiles=ALL):
            b, t, h = slices[s]
            rows = slice(tiles[0], tiles[-1] + 1)
            by_tile = live["result", s, tiles[0]][:].rearrange("p (j c) -> p j c", j=ROW_TILES)
            nc.sync.dma_start(
                out=out[b, t].rearrange("(p j) d -> p j d", j=ROW_TILES)[
                    :, rows, h * HD : (h + 1) * HD
                ],
                in_=by_tile[:, rows],
            )

        def average_on_gpsimd(s):
            b, t, h = slices[s]
            result = live["result", s, 0]
            by_tile = result[:].rearrange("p (j c) -> p j c", j=ROW_TILES)
            other = live["h_rows", b, t][:].rearrange("p (j d) -> p j d", j=ROW_TILES)
            nc.gpsimd.tensor_tensor(
                out=by_tile, in0=by_tile, in1=other[:, :, h * HD : (h + 1) * HD], op=ALU.add
            )
            nc.gpsimd.tensor_scalar(
                out=result[:], in0=result[:], scalar1=0.5, scalar2=0.0, op0=ALU.mult, op1=ALU.add
            )

        def average_on_vector(s, tiles=ALL):
            columns = slice(tiles[0] * HD, (tiles[-1] + 1) * HD)
            result = live["result", s, tiles[0]]
            nc.vector.scalar_tensor_tensor(
                out=result[:, columns],
                in0=result[:, columns],
                scalar=0.5,
                in1=live["half_h", s][:, columns],
                op0=ALU.mult,
                op1=ALU.add,
            )

        def finish(s):
            if is_slice(s):
                tanh_of_mean(s)
                average_on_gpsimd(s)
                store(s)

        load_q_and_k(0)
        load_bias()
        load_gate(0)
        load_weights()
        load_q_and_k(1)
        load_value(0)
        load_gate(1)
        load_q_and_k(2)
        load_gate(2)
        load_h(0)
        transpose_q_and_k(0)
        copy_q_and_k(0)
        score(0)
        score(1)
        spread_bias()
        transpose_weights(0)

        first_step = -1
        last = n_slices - 1
        value_step = {}
        for s in range(0, n_slices, H):
            value_step[max((s - 1) * ROW_TILES, 0)] = s
        for step in range(first_step, n_tiles):
            cur, j = divmod(step, ROW_TILES)

            if j == 0 and cur >= 0 and is_slice(cur + 3):
                load_q_and_k(cur + 3)
                load_gate(cur + 3)
            if j == 0 and starts_pair(cur + 3) and cur >= 0:
                load_value(cur + 3)
                load_h(cur + 3)

            if j == 2 and starts_pair(cur) and cur > 0:
                quantise_value(cur)

            if j == 0:
                if cur == last:
                    project_value(last)
                score(step + 2)
                attend(cur - 2)
                score(step + 3)
                transpose_e(cur - 1, HALVES[1])
            if j == 1 and step == 5:
                project_value(0)
            if j == 2:
                score(step + 2)
                if 1 <= cur < last:
                    project_value(cur)
                score(step + 3)
                transpose_e(cur, HALVES[0])
                transpose_q_and_k(cur + 2)
            if step == 0:
                transpose_q_and_k(1)
            if step in value_step:
                transpose_value(value_step[step], 0)
            if step - 2 in value_step:
                transpose_value(value_step[step - 2], 1)
            if step == 0:
                transpose_weights(1)

            if j == 0 and cur > 0 or step == 1:
                copy_q_and_k(cur + 1)
            if j == 1:
                copy_e(cur - 1, HALVES[1])
            if j == 2:
                finish(cur - 2)
            if j == 3:
                if 1 <= cur < last:
                    copy_v(cur)
                copy_e(cur, HALVES[0])
            if j == 0 and cur == last:
                copy_v(last)
            if step - 1 in value_step:
                copy_value(0)
            if step - 3 in value_step:
                copy_value(1)
            if step == -1:
                copy_weights(0)
            if step == 1:
                copy_weights(1)

            if j == 3 and 1 <= cur < last or j == 0 and cur == last:
                add_bias(cur)
            if j == 1 and cur in (last - 3, last - 2):
                halve_h(cur + 2)

            gate_scores(step + 1)
            row_max(step)
            if step == 4:
                quantise_value(0)
            if step == 5:
                add_bias(0)
            if j == 2:
                quantise_e(cur - 1)
                quantise_v(cur - 1)
            if j == 1 and cur >= 2 and cur % 2 == 0:
                invert_sums(cur // 2 - 1)
            if j == 1 and cur == last:
                invert_sums(last // 2, slice(0, 4))
            if step == 3:
                quantise_weights()

            exponentials(step)

        first = HALVES[0]
        attend(last - 1)
        tanh_of_mean(last - 1)
        transpose_e(last, [2])
        transpose_e(last, [3])
        copy_e(last, [2], nc.vector.tensor_copy)
        quantise_e(last, first)
        quantise_v(last)
        quantise_e(last, [2])
        invert_sums(last // 2, slice(4, 6))
        attend(last, first)
        tanh_of_mean(last, first)
        copy_e(last, [3], nc.vector.tensor_copy)
        invert_sums(last // 2, slice(6, 8))
        quantise_e(last, [3])
        average_on_vector(last - 1)
        store(last - 1)
        average_on_vector(last, first)
        store(last, first)
        for tiles in [2], [3]:
            attend(last, tiles)
            tanh_of_mean(last, tiles)
            average_on_vector(last, tiles)
            store(last, tiles)
